import numpy as np
import ml_dtypes


def mxq(x, axis, fmt="e4m3"):
    dtype, down = {"e4m3": (ml_dtypes.float8_e4m3fn, 7), "e5m2": (ml_dtypes.float8_e5m2, 14)}[fmt]
    v = np.moveaxis(np.asarray(x, np.float32).astype(ml_dtypes.bfloat16).astype(np.float64), axis, -1)
    blocks = v.reshape(v.shape[:-1] + (-1, 32))
    amax = np.abs(blocks).max(-1, keepdims=True)
    byte = np.maximum(np.where(amax > 0, np.frexp(amax)[1] - 1 + 127, 0) - down, 1)
    scale = np.exp2(byte - 127.0)
    codes = (blocks / scale).astype(np.float32).astype(dtype).astype(np.float64)
    return np.moveaxis((codes * scale).reshape(v.shape), -1, axis)


WIDE = False


def mx_kscale(k):
    if not WIDE:
        return np.ones(k)
    levels = np.array([10, -10, 5, -5, 0])
    if k % 512:
        return np.exp2(np.random.permutation(np.resize(levels, k // 32))).repeat(32)
    a = np.empty((k // 512, 16))
    for p in range(k // 512):
        a[p, :8] = np.random.permutation(np.resize(levels, 8))
        for g in range(8):
            far = levels[np.abs(levels - a[p, g]) >= 10]
            a[p, g + 8] = far[np.random.randint(len(far))]
    return np.exp2(a.ravel()).repeat(32)


BF16 = ml_dtypes.bfloat16


def bf(x):
    return np.asarray(x, np.float32).astype(BF16)


def f64(x):
    return np.asarray(x).astype(np.float64)


B, C, H, W, P, DIM = 8, 8, 128, 128, 16, 768
SHIFT = P // 2
PD = 5 * C * P * P
EPS = 1e-5
XS = 0.015


def patch_shift(x, shift):
    xp = np.pad(x, ((0, 0), (0, 0), (shift, shift), (shift, shift)))
    s2 = 2 * shift
    return np.concatenate([x, xp[:, :, :-s2, :-s2], xp[:, :, :-s2, s2:], xp[:, :, s2:, :-s2], xp[:, :, s2:, s2:]], axis=1)


def patchify(x, p):
    b_, c_, hh, ww = x.shape
    h, w = hh // p, ww // p
    return x.reshape(b_, c_, h, p, w, p).transpose(0, 2, 4, 3, 5, 1).reshape(b_, h * w, p * p * c_)


def layernorm(u, g, b):
    m = u.mean(-1, keepdims=True)
    v = np.square(u - m).mean(-1, keepdims=True)
    return (u - m) / np.sqrt(v + EPS) * g + b


def setup_inputs():
    s = mx_kscale(PD)
    return {"x": bf(np.random.standard_normal((B, C, H, W)) * XS),
            "ln1_g": bf((1.0 + 0.1 * np.random.standard_normal(PD)) * s),
            "ln1_b": bf(0.1 * np.random.standard_normal(PD) * s),
            "w1": bf(np.random.standard_normal((PD, DIM)) / np.sqrt(PD) / s[:, None]),
            "b1": bf(0.3 * np.random.standard_normal(DIM))}


def reference(x, ln1_g, ln1_b, w1, b1):
    u = patchify(patch_shift(f64(x), SHIFT), P)
    z = layernorm(u, f64(ln1_g), f64(ln1_b))
    return (mxq(z, 2, "e4m3") @ mxq(f64(w1), 0, "e4m3")) + f64(b1)

@@ -1,0 +1,307 @@
+from contextlib import ExitStack
+
+import concourse.mybir as mybir
+from concourse.masks import make_identity
+
+F32 = mybir.dt.float32
+BF16 = mybir.dt.bfloat16
+U32 = mybir.dt.uint32
+U8 = mybir.dt.uint8
+FP8X4 = mybir.dt.float8_e4m3fn_x4
+ALU = mybir.AluOpType
+ACT = mybir.ActivationFunctionType
+AX = mybir.AxisListType
+
+P = 128
+B, C, HW, DIM = 8, 8, 128, 768
+PD = 10240
+EPS = 1e-5
+FLOPS = 2 * B * 64 * PD * DIM
+SHIFTS = ((0, 0), (-1, -1), (-1, 1), (1, -1), (1, 1))
+PASSES = 20
+UNITS = 20
+HEAD_PASSES = 2
+LEAD_TILES = 5
+HEAD_SCALAR_COLS = 256
+BODY_SCALAR_COLS = 96
+
+
+def tile_shiftedpatchtokenization_pa_kernel(tc, x, ln1_g, ln1_b, w1, b1, out):
+    nc = tc.nc
+    with ExitStack() as ctx:
+        ctx.enter_context(tc.manual_schedule())
+        consts = ctx.enter_context(tc.tile_pool(name="consts", bufs=1))
+        wraw_pool = ctx.enter_context(tc.tile_pool(name="wraw", bufs=3))
+        wi_pool = ctx.enter_context(tc.tile_pool(name="wi", bufs=2))
+        xh_pool = ctx.enter_context(tc.tile_pool(name="xh", bufs=8))
+        zp_pool = ctx.enter_context(tc.tile_pool(name="zp", bufs=2))
+        zi_pool = ctx.enter_context(tc.tile_pool(name="zi", bufs=2))
+        zc_pool = ctx.enter_context(tc.tile_pool(name="zc", bufs=3))
+        o_pool = ctx.enter_context(tc.tile_pool(name="o", bufs=2))
+        acc_pool = ctx.enter_context(tc.psum_pool(name="acc", bufs=1))
+        tp_pool = ctx.enter_context(tc.psum_pool(name="tp", bufs=4))
+
+        w_codes = [consts.tile([P, DIM], U32, name="wc%d" % g, align_bytes=64) for g in range(PASSES)]
+        w_scales = [consts.tile([P, DIM], U8, name="ws%d" % g, align_bytes=64) for g in range(PASSES)]
+        w_raw = {}
+        w_grouped = {}
+
+        def load_w(n):
+            if n < PASSES:
+                wr = wraw_pool.tile([P, 4, DIM], BF16, name="wr")
+                nc.sync.dma_start(out=wr[:], in_=w1[512 * n:512 * n + 512, :].rearrange("(p t) n -> p t n", t=4))
+                w_raw[n] = wr
+
+        def regroup4(copy, dst, src):
+            copy(out=dst.rearrange("p (c i) t -> p c t i", i=4), in_=src.rearrange("p t (c i) -> p c t i", i=4))
+
+        def regroup_w(n, scalar_cols):
+            wr = w_raw.pop(n)
+            wi = wi_pool.tile([P, DIM, 4], BF16, name="wi", align_bytes=64)
+            cut = DIM - scalar_cols
+            regroup4(nc.scalar.copy, wi[:, cut:DIM, :], wr[:, :, cut:DIM])
+            regroup4(nc.vector.tensor_copy, wi[:, 0:cut, :], wr[:, :, 0:cut])
+            w_grouped[n] = wi
+            load_w(n + 3)
+
+        def quantise_w(n):
+            flat = w_grouped.pop(n)[:].rearrange("p n t -> p (n t)")
+            for lo, hi in ((0, 512), (512, 768)):
+                nc.vector.quantize_mx(
+                    out=w_codes[n][:, lo:hi].bitcast(FP8X4), scales=w_scales[n][:, lo:hi], in_=flat[:, 4 * lo:4 * hi]
+                )
+
+        gb = consts.tile([P, 512], BF16, name="gb")
+        nc.vector.memset(gb[:], 0.0)
+        nc.scalar.dma_start(out=gb[0:20, :], in_=ln1_g.rearrange("(r k) -> r k", k=512))
+        nc.scalar.dma_start(out=gb[32:52, :], in_=ln1_b.rearrange("(r k) -> r k", k=512))
+        for n in range(HEAD_PASSES):
+            load_w(n)
+        xr = consts.tile([P, 4, 32, HW], BF16, name="xr")
+        nc.vector.memset(xr[:, :, 0:8, :], 0.0)
+        nc.gpsimd.memset(xr[:, :, 24:32, :], 0.0)
+        for i in range(8):
+            for odd in range(2):
+                first = 64 * odd + 32 * (i // 4) + i % 4
+                top, bottom = max(16 * i - 8, 0), min(16 * i + 24, HW)
+                r0 = top - (16 * i - 8)
+                nc.sync.dma_start(
+                    out=xr[first:first + 29:4, :, r0:r0 + bottom - top, :].rearrange("p c r w -> p c (r w)"),
+                    in_=x[:, odd:C:2, top:bottom, :].rearrange("b c r w -> b c (r w)"),
+                )
+        for n in range(HEAD_PASSES, 3):
+            load_w(n)
+        b1b = consts.tile([P, DIM], BF16, name="b1b")
+
+        eye = consts.tile([P, P], F32, name="eye")
+        make_identity(nc, eye[:])
+        perm = consts.tile([P, P], F32, name="perm")
+        nc.vector.tensor_copy(
+            out=perm[:].rearrange("p (o b q x) -> p o b q x", o=2, b=8, q=2), in_=eye[:].rearrange("p (o q b x) -> p o b q x", o=2, q=2, b=8)
+        )
+        same = consts.tile([P, 2, 64], F32, name="same")
+        upper = consts.tile([P, 2, 64], F32, name="upper")
+        lower = consts.tile([P, 2, 64], F32, name="lower")
+        eye2 = eye[:].rearrange("p (o m) -> p o m", o=2)
+        for o in range(2):
+            nc.vector.tensor_add(out=same[:, o, :], in0=eye2[:, 0, :], in1=eye2[:, 1, :])
+        same5 = same[:].rearrange("p o (q b x) -> p (o q) b x", q=2, b=8)
+        for dst, to, frm, edge_to, edge_from in ((upper, slice(0, 3), slice(1, 4), (0, 3), (1, 0)), (lower, slice(1, 4), slice(0, 3), (1, 0), (0, 3))):
+            dst5 = dst[:].rearrange("p o (q b x) -> p (o q) b x", q=2, b=8)
+            nc.vector.tensor_copy(out=dst[:], in_=same[:])
+            nc.vector.tensor_add(out=dst5[:, :, :, to], in0=dst5[:, :, :, to], in1=same5[:, :, :, frm])
+            for o in range(2):
+                there = dst5[:, 2 * o + edge_to[0], :, edge_to[1]]
+                nc.vector.tensor_add(out=there, in0=there, in1=same5[:, 2 * o + edge_from[0], :, edge_from[1]])
+        padded = consts.tile([P, 4, 18], F32, name="padded")
+        nc.vector.memset(padded[:], 0.0)
+
+        regroup_w(0, HEAD_SCALAR_COLS)
+        for n in range(1, HEAD_PASSES):
+            regroup_w(n, HEAD_SCALAR_COLS)
+            quantise_w(n - 1)
+
+        gk = consts.tile([P, 4, PASSES], F32, name="gk")
+        bk = consts.tile([P, 4, PASSES], F32, name="bk")
+        gb_t = consts.tile([P, 4, P], F32, name="gb_t")
+        nc.vector.tensor_copy(out=gb_t[:], in_=gb[:].rearrange("r (p t) -> r t p", t=4))
+        pt = tp_pool.tile([P, 4, P], F32, name="tp")
+        for t in range(4):
+            nc.tensor.transpose(out=pt[:, t, :], in_=gb_t[:, t, :], identity=eye[:])
+        nc.vector.tensor_copy(out=gk[:], in_=pt[:, :, 0:20])
+        nc.vector.tensor_copy(out=bk[:], in_=pt[:, :, 32:52])
+        quantise_w(HEAD_PASSES - 1)
+
+        st6 = consts.tile([P, 2, 16, 6], F32, name="st6")
+        for a in range(2):
+            for j in range(16):
+                nc.vector.bn_stats(out=st6[:, a, j, :], in_=xr[:, :, 8 + 8 * a:16 + 8 * a, 8 * j:8 * j + 8])
+        groups = st6[:].rearrange("p a j (e k) -> p a j e k", e=2)
+        cells = consts.tile([P, 2, 2, 16], F32, name="cells")
+        sqm = consts.tile([P, 2, 16, 2], F32, name="sqm")
+        s2 = consts.tile([P, 2, 16], F32, name="s2")
+        m2 = consts.tile([P, 2, 16], F32, name="m2")
+        nc.vector.tensor_reduce(out=cells[:, :, 0, :], in_=groups[:, :, :, :, 1], axis=AX.X, op=ALU.add)
+        nc.vector.tensor_mul(out=sqm[:], in0=groups[:, :, :, :, 1], in1=groups[:, :, :, :, 1])
+        nc.vector.tensor_reduce(out=m2[:], in_=groups[:, :, :, :, 2], axis=AX.X, op=ALU.add)
+        nc.vector.tensor_reduce(out=s2[:], in_=sqm[:], axis=AX.X, op=ALU.add)
+        nc.vector.scalar_tensor_tensor(out=cells[:, :, 1, :], in0=s2[:], scalar=128.0, in1=m2[:], op0=ALU.mult, op1=ALU.add)
+        st = tp_pool.tile([P, 4, P], F32, name="tp")
+        for cols, over_upper, over_lower in ((slice(0, 32), upper, lower), (slice(32, 64), same, same)):
+            for a, rows in enumerate((over_upper, over_lower)):
+                nc.tensor.matmul(
+                    out=st[:, 0, cols],
+                    lhsT=rows[:].rearrange("p o m -> p (o m)"),
+                    rhs=cells[:, a, :, :].rearrange("p s j -> p (s j)"),
+                    start=(a == 0),
+                    stop=(a == 1),
+                )
+        nc.vector.tensor_copy(out=padded[:, :, 1:17], in_=st[:, 0, 0:64].rearrange("p (k j) -> p k j", j=16))
+        pairs = consts.tile([P, 2, 9], F32, name="pairs")
+        inner = consts.tile([P, 2, 8], F32, name="inner")
+        tot = consts.tile([P, 2, 8], F32, name="tot")
+        nc.vector.tensor_add(out=pairs[:], in0=padded[:, 0:2, 0:18:2], in1=padded[:, 0:2, 1:18:2])
+        nc.vector.tensor_add(out=inner[:], in0=padded[:, 2:4, 1:17:2], in1=padded[:, 2:4, 2:18:2])
+        nc.vector.tensor_add(out=tot[:], in0=pairs[:, :, 0:8], in1=pairs[:, :, 1:9])
+        nc.vector.tensor_add(out=tot[:], in0=tot[:], in1=inner[:])
+        small = {}
+        for nm in ("mean", "msq", "var", "std", "r0", "nt", "rstd", "nmr"):
+            small[nm] = consts.tile([P, 8], F32, name=nm)
+        mean, msq, var, std, r0, nt, rstd, nmr = (small[nm] for nm in ("mean", "msq", "var", "std", "r0", "nt", "rstd", "nmr"))
+        nc.vector.tensor_scalar_mul(out=mean[:], in0=tot[:, 0, :], scalar1=128.0 / PD)
+        nc.vector.tensor_mul(out=msq[:], in0=mean[:], in1=mean[:])
+        nc.vector.scalar_tensor_tensor(out=var[:], in0=tot[:, 1, :], scalar=1.0 / PD, in1=msq[:], op0=ALU.mult, op1=ALU.subtract)
+        nc.vector.tensor_scalar(out=var[:], in0=var[:], scalar1=0.0, scalar2=EPS, op0=ALU.max, op1=ALU.add)
+        nc.scalar.sqrt(out=std[:], in_=var[:])
+        nc.vector.reciprocal(out=r0[:], in_=std[:])
+        nc.vector.tensor_mul(out=nt[:], in0=r0[:], in1=r0[:])
+        nc.vector.tensor_mul(out=nt[:], in0=nt[:], in1=var[:])
+        nc.vector.tensor_scalar(out=nt[:], in0=nt[:], scalar1=-0.5, scalar2=1.5, op0=ALU.mult, op1=ALU.add)
+        nc.vector.tensor_mul(out=rstd[:], in0=r0[:], in1=nt[:])
+        nc.vector.scalar_tensor_tensor(out=nmr[:], in0=mean[:], scalar=-1.0, in1=rstd[:], op0=ALU.mult, op1=ALU.mult)
+
+        def affine(on_scalar, dst, src, scale, bias):
+            if on_scalar:
+                nc.scalar.activation(out=dst, in_=src, func=ACT.Identity, bias=bias, scale=scale)
+            else:
+                nc.vector.tensor_scalar(out=dst, in0=src, scalar1=scale, scalar2=bias, op0=ALU.mult, op1=ALU.add)
+
+        xh_tiles = {}
+
+        def normalise(k, n_scalar):
+            j = 4 * (k // 16) + k % 4
+            row0 = 8 + 4 * ((k % 16) // 4)
+            xh = xh_pool.tile([P, 1280], F32, name="xh")
+            view = xh[:].rearrange("p (q e s c) -> p q e s c", q=4, e=16, s=5)
+            for s, (di, dj) in enumerate(SHIFTS):
+                col0 = 16 * j + 8 * dj
+                lo = 8 if col0 < 0 else 0
+                hi = 8 if col0 + 16 > HW else 16
+                on_scalar = s >= 5 - n_scalar
+                src = xr[:, :, row0 + 8 * di:row0 + 8 * di + 4, col0 + lo:col0 + hi].rearrange("p c q e -> p q e c")
+                affine(on_scalar, view[:, :, lo:hi, s, :], src, rstd[:, j:j + 1], nmr[:, j:j + 1])
+                if hi - lo < 16:
+                    affine(on_scalar, view[:, :, 8 - lo:24 - hi, s, :], src, 0.0, nmr[:, j:j + 1])
+            xh_tiles[k] = xh
+
+        banks, planes, grouped, z_codes, acc = {}, {}, {}, {}, {}
+
+        def transposes(u):
+            banks[u] = {}
+            for a in range(2):
+                g = 2 * u + a
+                for t2 in range(2):
+                    pt = tp_pool.tile([P, 4, P], F32, name="tp")
+                    for jj in range(4):
+                        lo = 256 * (g % 5) + t2
+                        nc.tensor.transpose(out=pt[:, jj, :], in_=xh_tiles[4 * (g // 5) + jj][:, lo:lo + 255:2], identity=perm[:])
+                    banks[u][a, t2] = pt
+
+        def evacuate(u):
+            zp = zp_pool.tile([P, 2, 4, 256], BF16, name="zp")
+            for (a, t2), pt in banks.pop(u).items():
+                g = (2 * u + a) % PASSES
+                for o in range(2):
+                    t = 2 * t2 + o
+                    affine(True, zp[:, a, t, :].rearrange("p (j m) -> p j m", j=4), pt[:, :, 64 * o:64 * o + 64],
+                           gk[:, t, g:g + 1], bk[:, t, g:g + 1])
+            planes[u] = zp
+
+        def regroup_z(u):
+            zi = zi_pool.tile([P, 2, 256, 4], BF16, name="zi", align_bytes=64)
+            nc.vector.tensor_copy(
+                out=zi[:].rearrange("p a (c i) t -> p a c t i", i=4), in_=planes.pop(u)[:].rearrange("p a t (c i) -> p a c t i", i=4)
+            )
+            grouped[u] = zi
+
+        def quantise_z(u):
+            zc = zc_pool.tile([P, 512], U32, name="zc", align_bytes=64)
+            zs = zc_pool.tile([P, 512], U8, name="zs", align_bytes=64)
+            nc.vector.quantize_mx(out=zc[:].bitcast(FP8X4), scales=zs[:], in_=grouped.pop(u)[:].rearrange("p a m t -> p (a m t)"))
+            z_codes[u] = (zc, zs)
+
+        def multiply(u):
+            mu = u % 10
+            if mu == 0:
+                for k in range(4):
+                    acc[k] = acc_pool.tile([P, 512], F32, name="acc%d" % k)
+            zc, zs = z_codes.pop(u)
+            for tt in range(2):
+                for a in range(2):
+                    g = 2 * mu + a
+                    cols = slice(256 * a + P * tt, 256 * a + P * tt + P)
+                    for dst, lo, hi in ((acc[2 * tt], 0, 512), (acc[2 * tt + 1], 512, 768)):
+                        nc.tensor.matmul_mx(
+                            out=dst[:, 0:hi - lo],
+                            lhsT=zc[:, cols].bitcast(FP8X4),
+                            lhsT_scale=zs[:, cols],
+                            rhs=w_codes[g][:, lo:hi].bitcast(FP8X4),
+                            rhs_scale=w_scales[g][:, lo:hi],
+                            start=(mu == 0 and a == 0),
+                            stop=(mu == 9 and a == 1),
+                        )
+
+        out_rows = out.rearrange("b (i j) n -> j (b i) n", j=8)
+
+        def finish(half):
+            for tt in range(2):
+                o = o_pool.tile([P, DIM], F32, name="o")
+                nc.vector.tensor_tensor(out=o[:, 0:512], in0=acc[2 * tt][:], in1=b1b[:, 0:512], op=ALU.add)
+                nc.vector.tensor_tensor(out=o[:, 512:768], in0=acc[2 * tt + 1][:, 0:256], in1=b1b[:, 512:768], op=ALU.add)
+                for jl in range(2):
+                    nc.sync.dma_start(out=out_rows[4 * half + 2 * tt + jl], in_=o[64 * jl:64 * jl + 64, :])
+
+        for k in range(LEAD_TILES):
+            normalise(k, 2)
+        made = LEAD_TILES
+        waiting = []
+
+        def then_quantise(job):
+            if waiting:
+                waiting.pop()()
+            if job is not None:
+                waiting.append(job)
+
+        for step in range(UNITS + 3):
+            passes = range(min(HEAD_PASSES + (3 * step + 1) // 2, PASSES), min(HEAD_PASSES + (3 * step + 4) // 2, PASSES))
+            if 2 <= step < UNITS + 2:
+                regroup_z(step - 2)
+                then_quantise(lambda u=step - 2: quantise_z(u))
+            for n in passes:
+                regroup_w(n, BODY_SCALAR_COLS)
+                then_quantise(lambda n=n: quantise_w(n))
+            if step == 8:
+                nc.sync.dma_start(out=b1b[:], in_=b1.partition_broadcast(P))
+            if 1 <= step < UNITS + 1:
+                evacuate(step - 1)
+            if step >= 3:
+                multiply(step - 3)
+                if step - 3 in (9, 19):
+                    finish((step - 3) // 10)
+            if step < UNITS:
+                transposes(step)
+            target = min(32, LEAD_TILES + (8 * (step + 1) + 2) // 5)
+            while made < target:
+                normalise(made, 1 + 2 * len(passes))
+                made += 1
+            then_quantise(None)

@@ -19,11 +19,12 @@ EPS = 1e-5
 FLOPS = 2 * B * 64 * PD * DIM
 SHIFTS = ((0, 0), (-1, -1), (-1, 1), (1, -1), (1, 1))
 PASSES = 20
-UNITS = 20
-HEAD_PASSES = 2
-LEAD_TILES = 5
-HEAD_SCALAR_COLS = 256
-BODY_SCALAR_COLS = 96
+N1, N2 = 256, 512
+ITEMS = 30
+FIRST = 10
+HEAD_ITEMS = 6
+TILES = 32
+LEAD_TILES = 8
 
 
 def tile_shiftedpatchtokenization_pa_kernel(tc, x, ln1_g, ln1_b, w1, b1, out):
@@ -31,65 +32,75 @@ def tile_shiftedpatchtokenization_pa_kernel(tc, x, ln1_g, ln1_b, w1, b1, out):
     with ExitStack() as ctx:
         ctx.enter_context(tc.manual_schedule())
         consts = ctx.enter_context(tc.tile_pool(name="consts", bufs=1))
-        wraw_pool = ctx.enter_context(tc.tile_pool(name="wraw", bufs=3))
-        wi_pool = ctx.enter_context(tc.tile_pool(name="wi", bufs=2))
-        xh_pool = ctx.enter_context(tc.tile_pool(name="xh", bufs=8))
+        wraw_pool = ctx.enter_context(tc.tile_pool(name="wraw", bufs=4))
+        wi_pool = ctx.enter_context(tc.tile_pool(name="wi", bufs=4))
+        wc_pool = ctx.enter_context(tc.tile_pool(name="wc", bufs=8))
+        xh_pool = ctx.enter_context(tc.tile_pool(name="xh", bufs=14))
         zp_pool = ctx.enter_context(tc.tile_pool(name="zp", bufs=2))
         zi_pool = ctx.enter_context(tc.tile_pool(name="zi", bufs=2))
-        zc_pool = ctx.enter_context(tc.tile_pool(name="zc", bufs=3))
-        o_pool = ctx.enter_context(tc.tile_pool(name="o", bufs=2))
+        zc_pool = ctx.enter_context(tc.tile_pool(name="zc", bufs=1))
         acc_pool = ctx.enter_context(tc.psum_pool(name="acc", bufs=1))
         tp_pool = ctx.enter_context(tc.psum_pool(name="tp", bufs=4))
 
-        w_codes = [consts.tile([P, DIM], U32, name="wc%d" % g, align_bytes=64) for g in range(PASSES)]
-        w_scales = [consts.tile([P, DIM], U8, name="ws%d" % g, align_bytes=64) for g in range(PASSES)]
-        w_raw = {}
-        w_grouped = {}
+        w_raw, w_grouped, w_codes = {}, {}, {}
 
         def load_w(n):
-            if n < PASSES:
-                wr = wraw_pool.tile([P, 4, DIM], BF16, name="wr")
-                nc.sync.dma_start(out=wr[:], in_=w1[512 * n:512 * n + 512, :].rearrange("(p t) n -> p t n", t=4))
-                w_raw[n] = wr
+            if n < FIRST:
+                wr = wraw_pool.tile([P, 2048], BF16, name="wr")
+                for h in range(2):
+                    g = 2 * n + h
+                    nc.sync.dma_start(
+                        out=wr[:, 1024 * h:1024 * h + 1024].rearrange("p (t n) -> p t n", t=4),
+                        in_=w1[512 * g:512 * g + 512, N2:DIM].rearrange("(p t) n -> p t n", t=4),
+                    )
+            else:
+                wr = xh_pool.tile([P, 2048], BF16, name="xh")
+                g = n - FIRST
+                nc.sync.dma_start(
+                    out=wr[:].rearrange("p (t n) -> p t n", t=4), in_=w1[512 * g:512 * g + 512, 0:N2].rearrange("(p t) n -> p t n", t=4)
+                )
+            w_raw[n] = wr
 
         def regroup4(copy, dst, src):
             copy(out=dst.rearrange("p (c i) t -> p c t i", i=4), in_=src.rearrange("p t (c i) -> p c t i", i=4))
 
         def regroup_w(n, scalar_cols):
             wr = w_raw.pop(n)
-            wi = wi_pool.tile([P, DIM, 4], BF16, name="wi", align_bytes=64)
-            cut = DIM - scalar_cols
-            regroup4(nc.scalar.copy, wi[:, cut:DIM, :], wr[:, :, cut:DIM])
-            regroup4(nc.vector.tensor_copy, wi[:, 0:cut, :], wr[:, :, 0:cut])
+            wi = wi_pool.tile([P, 512, 4], BF16, name="wi", align_bytes=64)
+            width = N1 if n < FIRST else N2
+            for copy, start, stop in ((nc.scalar.copy, 512 - scalar_cols, 512), (nc.vector.tensor_copy, 0, 512 - scalar_cols)):
+                for first in range(0, 512, width):
+                    lo, hi = max(start, first), min(stop, first + width)
+                    if lo < hi:
+                        part = wr[:, 4 * first:4 * first + 4 * width].rearrange("p (t n) -> p t n", t=4)
+                        regroup4(copy, wi[:, lo:hi, :], part[:, :, lo - first:hi - first])
             w_grouped[n] = wi
-            load_w(n + 3)
+            if n + 4 < FIRST:
+                load_w(n + 4)
 
         def quantise_w(n):
-            flat = w_grouped.pop(n)[:].rearrange("p n t -> p (n t)")
-            for lo, hi in ((0, 512), (512, 768)):
-                nc.vector.quantize_mx(
-                    out=w_codes[n][:, lo:hi].bitcast(FP8X4), scales=w_scales[n][:, lo:hi], in_=flat[:, 4 * lo:4 * hi]
-                )
+            wc = wc_pool.tile([P, 512], U32, name="wc", align_bytes=64)
+            ws = wc_pool.tile([P, 512], U8, name="ws", align_bytes=64)
+            nc.vector.quantize_mx(out=wc[:].bitcast(FP8X4), scales=ws[:], in_=w_grouped.pop(n)[:].rearrange("p n t -> p (n t)"))
+            w_codes[n] = (wc, ws)
+
+        one = consts.tile([P, 1], F32, name="one")
+        nc.vector.memset(one[:], 1.0)
+        nc.scalar.activation(out=one[:], in_=one[:], func=ACT.Abs_reciprocal_sqrt)
 
         gb = consts.tile([P, 512], BF16, name="gb")
         nc.vector.memset(gb[:], 0.0)
         nc.scalar.dma_start(out=gb[0:20, :], in_=ln1_g.rearrange("(r k) -> r k", k=512))
         nc.scalar.dma_start(out=gb[32:52, :], in_=ln1_b.rearrange("(r k) -> r k", k=512))
-        for n in range(HEAD_PASSES):
-            load_w(n)
+        load_w(0)
         xr = consts.tile([P, 4, 32, HW], BF16, name="xr")
-        nc.vector.memset(xr[:, :, 0:8, :], 0.0)
-        nc.gpsimd.memset(xr[:, :, 24:32, :], 0.0)
-        for i in range(8):
-            for odd in range(2):
-                first = 64 * odd + 32 * (i // 4) + i % 4
-                top, bottom = max(16 * i - 8, 0), min(16 * i + 24, HW)
-                r0 = top - (16 * i - 8)
+        for half in range(4):
+            for b in (half, half + 4):
                 nc.sync.dma_start(
-                    out=xr[first:first + 29:4, :, r0:r0 + bottom - top, :].rearrange("p c r w -> p c (r w)"),
-                    in_=x[:, odd:C:2, top:bottom, :].rearrange("b c r w -> b c (r w)"),
+                    out=xr[b:b + 121:8, :, 8:24, :].rearrange("p c r w -> p c (r w)"),
+                    in_=x[b].rearrange("(c o) (i q) w -> (o i) c (q w)", o=2, i=8),
                 )
-        for n in range(HEAD_PASSES, 3):
+        for n in range(1, 4):
             load_w(n)
         b1b = consts.tile([P, DIM], BF16, name="b1b")
 
@@ -97,29 +108,35 @@ def tile_shiftedpatchtokenization_pa_kernel(tc, x, ln1_g, ln1_b, w1, b1, out):
         make_identity(nc, eye[:])
         perm = consts.tile([P, P], F32, name="perm")
         nc.vector.tensor_copy(
-            out=perm[:].rearrange("p (o b q x) -> p o b q x", o=2, b=8, q=2), in_=eye[:].rearrange("p (o q b x) -> p o b q x", o=2, q=2, b=8)
+            out=perm[:].rearrange("p (o b i) -> p o b i", o=2, b=8), in_=eye[:].rearrange("p (o i b) -> p o b i", o=2, i=8)
         )
+        rot_dn = consts.tile([P, 2, 64], BF16, name="rot_dn")
+        rot_up = consts.tile([P, 2, 64], BF16, name="rot_up")
+        nc.vector.memset(rot_dn[:], 0.0)
+        nc.vector.memset(rot_up[:], 0.0)
+        eye2 = eye[:].rearrange("p (o m) -> p o m", o=2)
+        nc.vector.tensor_copy(out=rot_dn[:, :, 8:64], in_=eye2[:, :, 0:56])
+        nc.vector.tensor_copy(out=rot_up[:, :, 0:56], in_=eye2[:, :, 8:64])
         same = consts.tile([P, 2, 64], F32, name="same")
         upper = consts.tile([P, 2, 64], F32, name="upper")
         lower = consts.tile([P, 2, 64], F32, name="lower")
-        eye2 = eye[:].rearrange("p (o m) -> p o m", o=2)
         for o in range(2):
             nc.vector.tensor_add(out=same[:, o, :], in0=eye2[:, 0, :], in1=eye2[:, 1, :])
-        same5 = same[:].rearrange("p o (q b x) -> p (o q) b x", q=2, b=8)
-        for dst, to, frm, edge_to, edge_from in ((upper, slice(0, 3), slice(1, 4), (0, 3), (1, 0)), (lower, slice(1, 4), slice(0, 3), (1, 0), (0, 3))):
-            dst5 = dst[:].rearrange("p o (q b x) -> p (o q) b x", q=2, b=8)
-            nc.vector.tensor_copy(out=dst[:], in_=same[:])
-            nc.vector.tensor_add(out=dst5[:, :, :, to], in0=dst5[:, :, :, to], in1=same5[:, :, :, frm])
-            for o in range(2):
-                there = dst5[:, 2 * o + edge_to[0], :, edge_to[1]]
-                nc.vector.tensor_add(out=there, in0=there, in1=same5[:, 2 * o + edge_from[0], :, edge_from[1]])
-        padded = consts.tile([P, 4, 18], F32, name="padded")
-        nc.vector.memset(padded[:], 0.0)
+        nc.vector.tensor_copy(out=upper[:], in_=same[:])
+        nc.vector.tensor_copy(out=lower[:], in_=same[:])
+        nc.vector.tensor_add(out=upper[:, :, 0:56], in0=upper[:, :, 0:56], in1=same[:, :, 8:64])
+        nc.vector.tensor_add(out=lower[:, :, 8:64], in0=lower[:, :, 8:64], in1=same[:, :, 0:56])
+        weights = consts.tile([P, 2, 2, P], F32, name="weights")
+        cells = consts.tile([P, 2, 2, 18], F32, name="cells")
+        nc.vector.memset(cells[:], 0.0)
+        for a, rows in enumerate((upper, lower)):
+            flat = rows[:].rearrange("p o m -> p (o m)")
+            nc.vector.tensor_scalar_mul(out=weights[:, 0, a, :], in0=flat, scalar1=128.0 / PD)
+            nc.vector.scalar_tensor_tensor(
+                out=weights[:, 1, a, :], in0=same[:].rearrange("p o m -> p (o m)"), scalar=128.0 / PD, in1=weights[:, 0, a, :], op0=ALU.mult, op1=ALU.add
+            )
 
-        regroup_w(0, HEAD_SCALAR_COLS)
-        for n in range(1, HEAD_PASSES):
-            regroup_w(n, HEAD_SCALAR_COLS)
-            quantise_w(n - 1)
+        regroup_w(0, 256)
 
         gk = consts.tile([P, 4, PASSES], F32, name="gk")
         bk = consts.tile([P, 4, PASSES], F32, name="bk")
@@ -130,55 +147,63 @@ def tile_shiftedpatchtokenization_pa_kernel(tc, x, ln1_g, ln1_b, w1, b1, out):
             nc.tensor.transpose(out=pt[:, t, :], in_=gb_t[:, t, :], identity=eye[:])
         nc.vector.tensor_copy(out=gk[:], in_=pt[:, :, 0:20])
         nc.vector.tensor_copy(out=bk[:], in_=pt[:, :, 32:52])
-        quantise_w(HEAD_PASSES - 1)
+        quantise_w(0)
 
         st6 = consts.tile([P, 2, 16, 6], F32, name="st6")
         for a in range(2):
             for j in range(16):
                 nc.vector.bn_stats(out=st6[:, a, j, :], in_=xr[:, :, 8 + 8 * a:16 + 8 * a, 8 * j:8 * j + 8])
+        def neighbours(c, dst, rot, row):
+            ps = tp_pool.tile([P, 1024], BF16, name="tp")
+            rows = xr[:, c, row:row + 8, :].rearrange("p r w -> p (r w)")
+            for h in range(2):
+                nc.tensor.matmul(
+                    out=ps[:, 512 * h:512 * h + 512], lhsT=rot[:].rearrange("p o m -> p (o m)"), rhs=rows[:, 512 * h:512 * h + 512],
+                    start=True, stop=True,
+                )
+            nc.scalar.copy(out=xr[:, c, dst:dst + 8, :].rearrange("p r w -> p (r w)"), in_=ps[:])
+
+        for c in range(4):
+            neighbours(c, 0, rot_dn, 16)
+        for n in range(1, 4):
+            regroup_w(n, 512)
         groups = st6[:].rearrange("p a j (e k) -> p a j e k", e=2)
-        cells = consts.tile([P, 2, 2, 16], F32, name="cells")
         sqm = consts.tile([P, 2, 16, 2], F32, name="sqm")
         s2 = consts.tile([P, 2, 16], F32, name="s2")
         m2 = consts.tile([P, 2, 16], F32, name="m2")
-        nc.vector.tensor_reduce(out=cells[:, :, 0, :], in_=groups[:, :, :, :, 1], axis=AX.X, op=ALU.add)
         nc.vector.tensor_mul(out=sqm[:], in0=groups[:, :, :, :, 1], in1=groups[:, :, :, :, 1])
         nc.vector.tensor_reduce(out=m2[:], in_=groups[:, :, :, :, 2], axis=AX.X, op=ALU.add)
         nc.vector.tensor_reduce(out=s2[:], in_=sqm[:], axis=AX.X, op=ALU.add)
-        nc.vector.scalar_tensor_tensor(out=cells[:, :, 1, :], in0=s2[:], scalar=128.0, in1=m2[:], op0=ALU.mult, op1=ALU.add)
-        st = tp_pool.tile([P, 4, P], F32, name="tp")
-        for cols, over_upper, over_lower in ((slice(0, 32), upper, lower), (slice(32, 64), same, same)):
-            for a, rows in enumerate((over_upper, over_lower)):
-                nc.tensor.matmul(
-                    out=st[:, 0, cols],
-                    lhsT=rows[:].rearrange("p o m -> p (o m)"),
-                    rhs=cells[:, a, :, :].rearrange("p s j -> p (s j)"),
-                    start=(a == 0),
-                    stop=(a == 1),
-                )
-        nc.vector.tensor_copy(out=padded[:, :, 1:17], in_=st[:, 0, 0:64].rearrange("p (k j) -> p k j", j=16))
-        pairs = consts.tile([P, 2, 9], F32, name="pairs")
-        inner = consts.tile([P, 2, 8], F32, name="inner")
+        nc.vector.tensor_reduce(out=cells[:, :, 0, 1:17], in_=groups[:, :, :, :, 1], axis=AX.X, op=ALU.add)
+        nc.vector.scalar_tensor_tensor(out=cells[:, :, 1, 1:17], in0=m2[:], scalar=1.0 / 128, in1=s2[:], op0=ALU.mult, op1=ALU.add)
+        columns = consts.tile([P, 2, 2, 2, 8], F32, name="columns")
+        for a in range(2):
+            nc.vector.tensor_add(out=columns[:, 0, a, :, :], in0=cells[:, a, :, 0:16:2], in1=cells[:, a, :, 3:18:2])
+            nc.vector.tensor_add(out=columns[:, 1, a, :, :], in0=cells[:, a, :, 1:17:2], in1=cells[:, a, :, 2:18:2])
+        st = tp_pool.tile([P, 2, 8], F32, name="tp")
+        for n in range(4):
+            nc.tensor.matmul(
+                out=st[:].rearrange("p s j -> p (s j)"),
+                lhsT=weights[:, n // 2, n % 2, :],
+                rhs=columns[:, n // 2, n % 2, :, :].rearrange("p s j -> p (s j)"),
+                start=(n == 0),
+                stop=(n == 3),
+            )
+        quantise_w(1)
         tot = consts.tile([P, 2, 8], F32, name="tot")
-        nc.vector.tensor_add(out=pairs[:], in0=padded[:, 0:2, 0:18:2], in1=padded[:, 0:2, 1:18:2])
-        nc.vector.tensor_add(out=inner[:], in0=padded[:, 2:4, 1:17:2], in1=padded[:, 2:4, 2:18:2])
-        nc.vector.tensor_add(out=tot[:], in0=pairs[:, :, 0:8], in1=pairs[:, :, 1:9])
-        nc.vector.tensor_add(out=tot[:], in0=tot[:], in1=inner[:])
         small = {}
-        for nm in ("mean", "msq", "var", "std", "r0", "nt", "rstd", "nmr"):
+        for nm in ("msq", "var", "r0", "nt", "rstd", "nmr"):
             small[nm] = consts.tile([P, 8], F32, name=nm)
-        mean, msq, var, std, r0, nt, rstd, nmr = (small[nm] for nm in ("mean", "msq", "var", "std", "r0", "nt", "rstd", "nmr"))
-        nc.vector.tensor_scalar_mul(out=mean[:], in0=tot[:, 0, :], scalar1=128.0 / PD)
-        nc.vector.tensor_mul(out=msq[:], in0=mean[:], in1=mean[:])
-        nc.vector.scalar_tensor_tensor(out=var[:], in0=tot[:, 1, :], scalar=1.0 / PD, in1=msq[:], op0=ALU.mult, op1=ALU.subtract)
-        nc.vector.tensor_scalar(out=var[:], in0=var[:], scalar1=0.0, scalar2=EPS, op0=ALU.max, op1=ALU.add)
-        nc.scalar.sqrt(out=std[:], in_=var[:])
-        nc.vector.reciprocal(out=r0[:], in_=std[:])
-        nc.vector.tensor_mul(out=nt[:], in0=r0[:], in1=r0[:])
+        msq, var, r0, nt, rstd, nmr = (small[nm] for nm in ("msq", "var", "r0", "nt", "rstd", "nmr"))
+        nc.vector.tensor_copy(out=tot[:], in_=st[:])
+        nc.vector.tensor_mul(out=msq[:], in0=tot[:, 0, :], in1=tot[:, 0, :])
+        nc.vector.scalar_tensor_tensor(out=var[:], in0=tot[:, 1, :], scalar=EPS, in1=msq[:], op0=ALU.add, op1=ALU.subtract)
+        nc.vector.tensor_scalar_max(out=var[:], in0=var[:], scalar1=EPS)
+        nc.scalar.activation(out=r0[:], in_=var[:], func=ACT.Abs_reciprocal_sqrt)
+        nc.vector.scalar_tensor_tensor(out=nt[:], in0=r0[:], scalar=-0.5, in1=r0[:], op0=ALU.mult, op1=ALU.mult)
         nc.vector.tensor_mul(out=nt[:], in0=nt[:], in1=var[:])
-        nc.vector.tensor_scalar(out=nt[:], in0=nt[:], scalar1=-0.5, scalar2=1.5, op0=ALU.mult, op1=ALU.add)
-        nc.vector.tensor_mul(out=rstd[:], in0=r0[:], in1=nt[:])
-        nc.vector.scalar_tensor_tensor(out=nmr[:], in0=mean[:], scalar=-1.0, in1=rstd[:], op0=ALU.mult, op1=ALU.mult)
+        nc.vector.scalar_tensor_tensor(out=rstd[:], in0=nt[:], scalar=1.5, in1=r0[:], op0=ALU.add, op1=ALU.mult)
+        nc.vector.scalar_tensor_tensor(out=nmr[:], in0=tot[:, 0, :], scalar=-1.0, in1=rstd[:], op0=ALU.mult, op1=ALU.mult)
 
         def affine(on_scalar, dst, src, scale, bias):
             if on_scalar:
@@ -189,8 +214,8 @@ def tile_shiftedpatchtokenization_pa_kernel(tc, x, ln1_g, ln1_b, w1, b1, out):
         xh_tiles = {}
 
         def normalise(k, n_scalar):
-            j = 4 * (k // 16) + k % 4
-            row0 = 8 + 4 * ((k % 16) // 4)
+            j = k % 8
+            row0 = 8 + 4 * (k // 8)
             xh = xh_pool.tile([P, 1280], F32, name="xh")
             view = xh[:].rearrange("p (q e s c) -> p q e s c", q=4, e=16, s=5)
             for s, (di, dj) in enumerate(SHIFTS):
@@ -204,104 +229,118 @@ def tile_shiftedpatchtokenization_pa_kernel(tc, x, ln1_g, ln1_b, w1, b1, out):
                     affine(on_scalar, view[:, :, 8 - lo:24 - hi, s, :], src, 0.0, nmr[:, j:j + 1])
             xh_tiles[k] = xh
 
-        banks, planes, grouped, z_codes, acc = {}, {}, {}, {}, {}
+        banks, planes, grouped, z_codes = {}, {}, {}, {}
 
-        def transposes(u):
-            banks[u] = {}
-            for a in range(2):
-                g = 2 * u + a
+        def transposes(g):
+            banks[g] = {}
+            for jg in range(2):
                 for t2 in range(2):
                     pt = tp_pool.tile([P, 4, P], F32, name="tp")
                     for jj in range(4):
                         lo = 256 * (g % 5) + t2
-                        nc.tensor.transpose(out=pt[:, jj, :], in_=xh_tiles[4 * (g // 5) + jj][:, lo:lo + 255:2], identity=perm[:])
-                    banks[u][a, t2] = pt
+                        xh = xh_tiles[8 * (g // 5) + 4 * jg + jj]
+                        nc.tensor.transpose(out=pt[:, jj, :], in_=xh[:, lo:lo + 255:2], identity=perm[:])
+                    banks[g][jg, t2] = pt
 
-        def evacuate(u):
-            zp = zp_pool.tile([P, 2, 4, 256], BF16, name="zp")
-            for (a, t2), pt in banks.pop(u).items():
-                g = (2 * u + a) % PASSES
+        def evacuate(g):
+            zp = zp_pool.tile([P, 4, 512], BF16, name="zp")
+            for (jg, t2), pt in banks.pop(g).items():
                 for o in range(2):
                     t = 2 * t2 + o
-                    affine(True, zp[:, a, t, :].rearrange("p (j m) -> p j m", j=4), pt[:, :, 64 * o:64 * o + 64],
+                    affine(True, zp[:, t, 256 * jg:256 * jg + 256].rearrange("p (j m) -> p j m", j=4), pt[:, :, 64 * o:64 * o + 64],
                            gk[:, t, g:g + 1], bk[:, t, g:g + 1])
-            planes[u] = zp
+            planes[g] = zp
 
-        def regroup_z(u):
-            zi = zi_pool.tile([P, 2, 256, 4], BF16, name="zi", align_bytes=64)
-            nc.vector.tensor_copy(
-                out=zi[:].rearrange("p a (c i) t -> p a c t i", i=4), in_=planes.pop(u)[:].rearrange("p a t (c i) -> p a c t i", i=4)
-            )
-            grouped[u] = zi
+        def regroup_z(g):
+            zi = zi_pool.tile([P, 512, 4], BF16, name="zi", align_bytes=64)
+            regroup4(nc.vector.tensor_copy, zi[:], planes.pop(g)[:])
+            grouped[g] = zi
 
-        def quantise_z(u):
-            zc = zc_pool.tile([P, 512], U32, name="zc", align_bytes=64)
-            zs = zc_pool.tile([P, 512], U8, name="zs", align_bytes=64)
-            nc.vector.quantize_mx(out=zc[:].bitcast(FP8X4), scales=zs[:], in_=grouped.pop(u)[:].rearrange("p a m t -> p (a m t)"))
-            z_codes[u] = (zc, zs)
+        def quantise_z(g):
+            zc = zc_pool.tile([P, 512], U32, name="zc%d" % g, align_bytes=64)
+            zs = zc_pool.tile([P, 512], U8, name="zs%d" % g, align_bytes=64)
+            nc.vector.quantize_mx(out=zc[:].bitcast(FP8X4), scales=zs[:], in_=grouped.pop(g)[:].rearrange("p m t -> p (m t)"))
+            z_codes[g] = (zc, zs)
 
-        def multiply(u):
-            mu = u % 10
-            if mu == 0:
-                for k in range(4):
-                    acc[k] = acc_pool.tile([P, 512], F32, name="acc%d" % k)
-            zc, zs = z_codes.pop(u)
-            for tt in range(2):
-                for a in range(2):
-                    g = 2 * mu + a
-                    cols = slice(256 * a + P * tt, 256 * a + P * tt + P)
-                    for dst, lo, hi in ((acc[2 * tt], 0, 512), (acc[2 * tt + 1], 512, 768)):
-                        nc.tensor.matmul_mx(
-                            out=dst[:, 0:hi - lo],
-                            lhsT=zc[:, cols].bitcast(FP8X4),
-                            lhsT_scale=zs[:, cols],
-                            rhs=w_codes[g][:, lo:hi].bitcast(FP8X4),
-                            rhs_scale=w_scales[g][:, lo:hi],
-                            start=(mu == 0 and a == 0),
-                            stop=(mu == 9 and a == 1),
-                        )
+        def multiply(acc, g, codes, first, width):
+            zc, zs = z_codes[g]
+            wc, ws = codes
+            for tt in range(4):
+                nc.tensor.matmul_mx(
+                    out=acc[tt][:, 0:width],
+                    lhsT=zc[:, P * tt:P * tt + P].bitcast(FP8X4),
+                    lhsT_scale=zs[:, P * tt:P * tt + P],
+                    rhs=wc[:, first:first + width].bitcast(FP8X4),
+                    rhs_scale=ws[:, first:first + width],
+                    start=(g == 0),
+                    stop=(g == PASSES - 1),
+                )
 
         out_rows = out.rearrange("b (i j) n -> j (b i) n", j=8)
 
-        def finish(half):
-            for tt in range(2):
-                o = o_pool.tile([P, DIM], F32, name="o")
-                nc.vector.tensor_tensor(out=o[:, 0:512], in0=acc[2 * tt][:], in1=b1b[:, 0:512], op=ALU.add)
-                nc.vector.tensor_tensor(out=o[:, 512:768], in0=acc[2 * tt + 1][:, 0:256], in1=b1b[:, 512:768], op=ALU.add)
+        def finish(acc, first, width):
+            for tt in range(4):
+                o = wraw_pool.tile([P, N2], F32, name="wr")
+                nc.vector.tensor_tensor(out=o[:, 0:width], in0=acc[tt][:, 0:width], in1=b1b[:, first:first + width], op=ALU.add)
                 for jl in range(2):
-                    nc.sync.dma_start(out=out_rows[4 * half + 2 * tt + jl], in_=o[64 * jl:64 * jl + 64, :])
+                    nc.sync.dma_start(out=out_rows[2 * tt + jl][:, first:first + width], in_=o[64 * jl:64 * jl + 64, 0:width])
 
+        narrow, wide = {}, {}
+        for tt in range(4):
+            narrow[tt] = acc_pool.tile([P, N1], F32, name="acc%d" % tt)
         for k in range(LEAD_TILES):
-            normalise(k, 2)
+            normalise(k, 2 if k < 4 else 0)
         made = LEAD_TILES
-        waiting = []
-
-        def then_quantise(job):
-            if waiting:
-                waiting.pop()()
-            if job is not None:
-                waiting.append(job)
-
-        for step in range(UNITS + 3):
-            passes = range(min(HEAD_PASSES + (3 * step + 1) // 2, PASSES), min(HEAD_PASSES + (3 * step + 4) // 2, PASSES))
-            if 2 <= step < UNITS + 2:
+        quantise_w(2)
+        quantise_w(3)
+        for n in range(4, HEAD_ITEMS):
+            regroup_w(n, 0)
+            quantise_w(n)
+        next_item = HEAD_ITEMS
+        next_load = FIRST
+        for step in range(PASSES + 3):
+            if 1 <= step < PASSES + 1:
+                evacuate(step - 1)
+            if 1 <= step < 5:
+                neighbours(step - 1, 24, rot_up, 8)
+            if 2 <= step < PASSES + 2:
                 regroup_z(step - 2)
-                then_quantise(lambda u=step - 2: quantise_z(u))
-            for n in passes:
-                regroup_w(n, BODY_SCALAR_COLS)
-                then_quantise(lambda n=n: quantise_w(n))
+            items = range(next_item, min(HEAD_ITEMS + (step + 1) // 5, FIRST))
+            next_item += len(items)
+            for n in items:
+                regroup_w(n, 0)
+            if 2 <= step < PASSES + 2:
+                quantise_z(step - 2)
             if step == 8:
                 nc.sync.dma_start(out=b1b[:], in_=b1.partition_broadcast(P))
-            if 1 <= step < UNITS + 1:
-                evacuate(step - 1)
             if step >= 3:
-                multiply(step - 3)
-                if step - 3 in (9, 19):
-                    finish((step - 3) // 10)
-            if step < UNITS:
+                g = step - 3
+                multiply(narrow, g, w_codes[g // 2], N1 * (g % 2), N1)
+            if step < PASSES:
                 transposes(step)
-            target = min(32, LEAD_TILES + (8 * (step + 1) + 2) // 5)
+            target = min(TILES, LEAD_TILES + (8 * (step + 1)) // 5)
             while made < target:
-                normalise(made, 1 + 2 * len(passes))
+                normalise(made, 1)
                 made += 1
-            then_quantise(None)
+            if step in (15, 16):
+                for n in range(next_load, next_load + 3):
+                    load_w(n)
+                next_load += 3
+            for n in items:
+                quantise_w(n)
+        while next_load < FIRST + 14:
+            load_w(next_load)
+            next_load += 1
+        for tt in range(4):
+            wide[tt] = tp_pool.tile([P, N2], F32, name="tp")
+        for n in range(FIRST, ITEMS + 1):
+            if n < ITEMS:
+                regroup_w(n, 256)
+                if n + 14 < ITEMS:
+                    load_w(n + 14)
+            if n == FIRST + 1:
+                finish(narrow, N2, N1)
+            if n > FIRST:
+                quantise_w(n - 1)
+                multiply(wide, n - 1 - FIRST, w_codes.pop(n - 1), 0, N2)
+        finish(wide, 0, N2)

@@ -19,9 +19,9 @@ EPS = 1e-5
 FLOPS = 2 * B * 64 * PD * DIM
 SHIFTS = ((0, 0), (-1, -1), (-1, 1), (1, -1), (1, 1))
 PASSES = 20
-N1, N2 = 256, 512
+N1, N2 = 512, 256
 ITEMS = 30
-FIRST = 10
+FIRST = 20
 HEAD_ITEMS = 6
 TILES = 32
 LEAD_TILES = 8
@@ -34,7 +34,7 @@ def tile_shiftedpatchtokenization_pa_kernel(tc, x, ln1_g, ln1_b, w1, b1, out):
         consts = ctx.enter_context(tc.tile_pool(name="consts", bufs=1))
         wraw_pool = ctx.enter_context(tc.tile_pool(name="wraw", bufs=4))
         wi_pool = ctx.enter_context(tc.tile_pool(name="wi", bufs=4))
-        wc_pool = ctx.enter_context(tc.tile_pool(name="wc", bufs=8))
+        wc_pool = ctx.enter_context(tc.tile_pool(name="wc", bufs=9))
         xh_pool = ctx.enter_context(tc.tile_pool(name="xh", bufs=14))
         zp_pool = ctx.enter_context(tc.tile_pool(name="zp", bufs=2))
         zi_pool = ctx.enter_context(tc.tile_pool(name="zi", bufs=2))
@@ -47,18 +47,17 @@ def tile_shiftedpatchtokenization_pa_kernel(tc, x, ln1_g, ln1_b, w1, b1, out):
         def load_w(n):
             if n < FIRST:
                 wr = wraw_pool.tile([P, 2048], BF16, name="wr")
-                for h in range(2):
-                    g = 2 * n + h
-                    nc.sync.dma_start(
-                        out=wr[:, 1024 * h:1024 * h + 1024].rearrange("p (t n) -> p t n", t=4),
-                        in_=w1[512 * g:512 * g + 512, N2:DIM].rearrange("(p t) n -> p t n", t=4),
-                    )
+                nc.sync.dma_start(
+                    out=wr[:].rearrange("p (t n) -> p t n", t=4), in_=w1[512 * n:512 * n + 512, 0:N1].rearrange("(p t) n -> p t n", t=4)
+                )
             else:
                 wr = xh_pool.tile([P, 2048], BF16, name="xh")
-                g = n - FIRST
-                nc.sync.dma_start(
-                    out=wr[:].rearrange("p (t n) -> p t n", t=4), in_=w1[512 * g:512 * g + 512, 0:N2].rearrange("(p t) n -> p t n", t=4)
-                )
+                for h in range(2):
+                    g = 2 * (n - FIRST) + h
+                    nc.sync.dma_start(
+                        out=wr[:, 1024 * h:1024 * h + 1024].rearrange("p (t n) -> p t n", t=4),
+                        in_=w1[512 * g:512 * g + 512, N1:DIM].rearrange("(p t) n -> p t n", t=4),
+                    )
             w_raw[n] = wr
 
         def regroup4(copy, dst, src):
@@ -280,14 +279,14 @@ def tile_shiftedpatchtokenization_pa_kernel(tc, x, ln1_g, ln1_b, w1, b1, out):
 
         def finish(acc, first, width):
             for tt in range(4):
-                o = wraw_pool.tile([P, N2], F32, name="wr")
+                o = wraw_pool.tile([P, N1], F32, name="wr")
                 nc.vector.tensor_tensor(out=o[:, 0:width], in0=acc[tt][:, 0:width], in1=b1b[:, first:first + width], op=ALU.add)
                 for jl in range(2):
                     nc.sync.dma_start(out=out_rows[2 * tt + jl][:, first:first + width], in_=o[64 * jl:64 * jl + 64, 0:width])
 
-        narrow, wide = {}, {}
+        wide, narrow = {}, {}
         for tt in range(4):
-            narrow[tt] = acc_pool.tile([P, N1], F32, name="acc%d" % tt)
+            wide[tt] = acc_pool.tile([P, N1], F32, name="acc%d" % tt)
         for k in range(LEAD_TILES):
             normalise(k, 2 if k < 4 else 0)
         made = LEAD_TILES
@@ -305,17 +304,16 @@ def tile_shiftedpatchtokenization_pa_kernel(tc, x, ln1_g, ln1_b, w1, b1, out):
                 neighbours(step - 1, 24, rot_up, 8)
             if 2 <= step < PASSES + 2:
                 regroup_z(step - 2)
-            items = range(next_item, min(HEAD_ITEMS + (step + 1) // 5, FIRST))
+            items = range(next_item, min(HEAD_ITEMS + (7 * (step + 1)) // 10, FIRST))
             next_item += len(items)
             for n in items:
-                regroup_w(n, 0)
+                regroup_w(n, 256)
             if 2 <= step < PASSES + 2:
                 quantise_z(step - 2)
             if step == 8:
                 nc.sync.dma_start(out=b1b[:], in_=b1.partition_broadcast(P))
             if step >= 3:
-                g = step - 3
-                multiply(narrow, g, w_codes[g // 2], N1 * (g % 2), N1)
+                multiply(wide, step - 3, w_codes.pop(step - 3), 0, N1)
             if step < PASSES:
                 transposes(step)
             target = min(TILES, LEAD_TILES + (8 * (step + 1)) // 5)
@@ -328,19 +326,20 @@ def tile_shiftedpatchtokenization_pa_kernel(tc, x, ln1_g, ln1_b, w1, b1, out):
                 next_load += 3
             for n in items:
                 quantise_w(n)
-        while next_load < FIRST + 14:
+        while next_load < ITEMS:
             load_w(next_load)
             next_load += 1
+
         for tt in range(4):
-            wide[tt] = tp_pool.tile([P, N2], F32, name="tp")
+            narrow[tt] = tp_pool.tile([P, N2], F32, name="tp")
         for n in range(FIRST, ITEMS + 1):
             if n < ITEMS:
                 regroup_w(n, 256)
-                if n + 14 < ITEMS:
-                    load_w(n + 14)
             if n == FIRST + 1:
-                finish(narrow, N2, N1)
+                finish(wide, 0, N1)
             if n > FIRST:
                 quantise_w(n - 1)
-                multiply(wide, n - 1 - FIRST, w_codes.pop(n - 1), 0, N2)
-        finish(wide, 0, N2)
+                codes = w_codes.pop(n - 1)
+                for h in range(2):
+                    multiply(narrow, 2 * (n - 1 - FIRST) + h, codes, N2 * h, N2)
+        finish(narrow, N1, N2)

@@ -22,7 +22,8 @@ PASSES = 20
 N1, N2 = 512, 256
 ITEMS = 30
 FIRST = 20
-HEAD_ITEMS = 6
+HEAD_ITEMS = 9
+SLOTS = 24
 TILES = 32
 LEAD_TILES = 8
 
@@ -32,17 +33,19 @@ def tile_shiftedpatchtokenization_pa_kernel(tc, x, ln1_g, ln1_b, w1, b1, out):
     with ExitStack() as ctx:
         ctx.enter_context(tc.manual_schedule())
         consts = ctx.enter_context(tc.tile_pool(name="consts", bufs=1))
-        wraw_pool = ctx.enter_context(tc.tile_pool(name="wraw", bufs=4))
-        wi_pool = ctx.enter_context(tc.tile_pool(name="wi", bufs=4))
-        wc_pool = ctx.enter_context(tc.tile_pool(name="wc", bufs=9))
+        wraw_pool = ctx.enter_context(tc.tile_pool(name="wraw", bufs=5))
+        wi_pool = ctx.enter_context(tc.tile_pool(name="wi", bufs=6))
         xh_pool = ctx.enter_context(tc.tile_pool(name="xh", bufs=14))
         zp_pool = ctx.enter_context(tc.tile_pool(name="zp", bufs=2))
         zi_pool = ctx.enter_context(tc.tile_pool(name="zi", bufs=2))
-        zc_pool = ctx.enter_context(tc.tile_pool(name="zc", bufs=1))
         acc_pool = ctx.enter_context(tc.psum_pool(name="acc", bufs=1))
         tp_pool = ctx.enter_context(tc.psum_pool(name="tp", bufs=4))
 
         w_raw, w_grouped, w_codes = {}, {}, {}
+        free_slots = [
+            (consts.tile([P, 512], U32, name="codes%d" % n, align_bytes=64), consts.tile([P, 512], U8, name="scales%d" % n, align_bytes=64))
+            for n in range(SLOTS)
+        ]
 
         def load_w(n):
             if n < FIRST:
@@ -63,6 +66,26 @@ def tile_shiftedpatchtokenization_pa_kernel(tc, x, ln1_g, ln1_b, w1, b1, out):
         def regroup4(copy, dst, src):
             copy(out=dst.rearrange("p (c i) t -> p c t i", i=4), in_=src.rearrange("p t (c i) -> p c t i", i=4))
 
+        def regroup_w_head(n):
+            wr = w_raw.pop(n)[:].rearrange("p (t n) -> p t n", t=4)
+            wi = wi_pool.tile([P, 512, 4], BF16, name="wi", align_bytes=64)
+            for lo in range(0, 512, 256):
+                if n < 2:
+                    nc.gpsimd.tensor_scalar(
+                        out=wi[:, lo:lo + 256, :], in0=wr[:, :, lo:lo + 256].rearrange("p t n -> p n t"),
+                        scalar1=1.0, scalar2=0.0, op0=ALU.mult, op1=ALU.add,
+                    )
+                else:
+                    ps = tp_pool.tile([P, 256, 4], BF16, name="tp")
+                    for h in range(2):
+                        nc.tensor.matmul(
+                            out=ps[:, 128 * h:128 * h + 128, :].rearrange("p n t -> p (n t)"), lhsT=eye_bf[:],
+                            rhs=wr[:, :, lo + 128 * h:lo + 128 * h + 128].rearrange("p t n -> p n t"), start=True, stop=True,
+                        )
+                    nc.scalar.copy(out=wi[:, lo:lo + 256, :].rearrange("p n t -> p (n t)"), in_=ps[:].rearrange("p n t -> p (n t)"))
+            w_grouped[n] = wi
+            load_w(n + 5)
+
         def regroup_w(n, scalar_cols):
             wr = w_raw.pop(n)
             wi = wi_pool.tile([P, 512, 4], BF16, name="wi", align_bytes=64)
@@ -74,12 +97,11 @@ def tile_shiftedpatchtokenization_pa_kernel(tc, x, ln1_g, ln1_b, w1, b1, out):
                         part = wr[:, 4 * first:4 * first + 4 * width].rearrange("p (t n) -> p t n", t=4)
                         regroup4(copy, wi[:, lo:hi, :], part[:, :, lo - first:hi - first])
             w_grouped[n] = wi
-            if n + 4 < FIRST:
-                load_w(n + 4)
+            if n + 5 < FIRST:
+                load_w(n + 5)
 
         def quantise_w(n):
-            wc = wc_pool.tile([P, 512], U32, name="wc", align_bytes=64)
-            ws = wc_pool.tile([P, 512], U8, name="ws", align_bytes=64)
+            wc, ws = free_slots.pop(0)
             nc.vector.quantize_mx(out=wc[:].bitcast(FP8X4), scales=ws[:], in_=w_grouped.pop(n)[:].rearrange("p n t -> p (n t)"))
             w_codes[n] = (wc, ws)
 
@@ -91,7 +113,6 @@ def tile_shiftedpatchtokenization_pa_kernel(tc, x, ln1_g, ln1_b, w1, b1, out):
         nc.vector.memset(gb[:], 0.0)
         nc.scalar.dma_start(out=gb[0:20, :], in_=ln1_g.rearrange("(r k) -> r k", k=512))
         nc.scalar.dma_start(out=gb[32:52, :], in_=ln1_b.rearrange("(r k) -> r k", k=512))
-        load_w(0)
         xr = consts.tile([P, 4, 32, HW], BF16, name="xr")
         for half in range(4):
             for b in (half, half + 4):
@@ -99,12 +120,14 @@ def tile_shiftedpatchtokenization_pa_kernel(tc, x, ln1_g, ln1_b, w1, b1, out):
                     out=xr[b:b + 121:8, :, 8:24, :].rearrange("p c r w -> p c (r w)"),
                     in_=x[b].rearrange("(c o) (i q) w -> (o i) c (q w)", o=2, i=8),
                 )
-        for n in range(1, 4):
+        for n in range(5):
             load_w(n)
         b1b = consts.tile([P, DIM], BF16, name="b1b")
 
         eye = consts.tile([P, P], F32, name="eye")
         make_identity(nc, eye[:])
+        eye_bf = consts.tile([P, P], BF16, name="eye_bf")
+        nc.vector.tensor_copy(out=eye_bf[:], in_=eye[:])
         perm = consts.tile([P, P], F32, name="perm")
         nc.vector.tensor_copy(
             out=perm[:].rearrange("p (o b i) -> p o b i", o=2, b=8), in_=eye[:].rearrange("p (o i b) -> p o b i", o=2, i=8)
@@ -135,7 +158,8 @@ def tile_shiftedpatchtokenization_pa_kernel(tc, x, ln1_g, ln1_b, w1, b1, out):
                 out=weights[:, 1, a, :], in0=same[:].rearrange("p o m -> p (o m)"), scalar=128.0 / PD, in1=weights[:, 0, a, :], op0=ALU.mult, op1=ALU.add
             )
 
-        regroup_w(0, 256)
+        for n in range(2):
+            regroup_w_head(n)
 
         gk = consts.tile([P, 4, PASSES], F32, name="gk")
         bk = consts.tile([P, 4, PASSES], F32, name="bk")
@@ -146,7 +170,6 @@ def tile_shiftedpatchtokenization_pa_kernel(tc, x, ln1_g, ln1_b, w1, b1, out):
             nc.tensor.transpose(out=pt[:, t, :], in_=gb_t[:, t, :], identity=eye[:])
         nc.vector.tensor_copy(out=gk[:], in_=pt[:, :, 0:20])
         nc.vector.tensor_copy(out=bk[:], in_=pt[:, :, 32:52])
-        quantise_w(0)
 
         st6 = consts.tile([P, 2, 16, 6], F32, name="st6")
         for a in range(2):
@@ -164,8 +187,8 @@ def tile_shiftedpatchtokenization_pa_kernel(tc, x, ln1_g, ln1_b, w1, b1, out):
 
         for c in range(4):
             neighbours(c, 0, rot_dn, 16)
-        for n in range(1, 4):
-            regroup_w(n, 512)
+        for n in range(2, 5):
+            regroup_w_head(n)
         groups = st6[:].rearrange("p a j (e k) -> p a j e k", e=2)
         sqm = consts.tile([P, 2, 16, 2], F32, name="sqm")
         s2 = consts.tile([P, 2, 16], F32, name="s2")
@@ -188,6 +211,7 @@ def tile_shiftedpatchtokenization_pa_kernel(tc, x, ln1_g, ln1_b, w1, b1, out):
                 start=(n == 0),
                 stop=(n == 3),
             )
+        quantise_w(0)
         quantise_w(1)
         tot = consts.tile([P, 2, 8], F32, name="tot")
         small = {}
@@ -256,8 +280,7 @@ def tile_shiftedpatchtokenization_pa_kernel(tc, x, ln1_g, ln1_b, w1, b1, out):
             grouped[g] = zi
 
         def quantise_z(g):
-            zc = zc_pool.tile([P, 512], U32, name="zc%d" % g, align_bytes=64)
-            zs = zc_pool.tile([P, 512], U8, name="zs%d" % g, align_bytes=64)
+            zc, zs = free_slots.pop(0)
             nc.vector.quantize_mx(out=zc[:].bitcast(FP8X4), scales=zs[:], in_=grouped.pop(g)[:].rearrange("p m t -> p (m t)"))
             z_codes[g] = (zc, zs)
 
@@ -288,14 +311,16 @@ def tile_shiftedpatchtokenization_pa_kernel(tc, x, ln1_g, ln1_b, w1, b1, out):
         for tt in range(4):
             wide[tt] = acc_pool.tile([P, N1], F32, name="acc%d" % tt)
         for k in range(LEAD_TILES):
+            if k == 4:
+                for n in range(5, HEAD_ITEMS):
+                    quantise_w(n - 3)
+                    regroup_w_head(n)
             normalise(k, 2 if k < 4 else 0)
         made = LEAD_TILES
-        quantise_w(2)
-        quantise_w(3)
-        for n in range(4, HEAD_ITEMS):
-            regroup_w(n, 0)
+        for n in range(HEAD_ITEMS - 3, HEAD_ITEMS):
             quantise_w(n)
         next_item = HEAD_ITEMS
+        regrouped = []
         next_load = FIRST
         for step in range(PASSES + 3):
             if 1 <= step < PASSES + 1:
@@ -304,16 +329,21 @@ def tile_shiftedpatchtokenization_pa_kernel(tc, x, ln1_g, ln1_b, w1, b1, out):
                 neighbours(step - 1, 24, rot_up, 8)
             if 2 <= step < PASSES + 2:
                 regroup_z(step - 2)
-            items = range(next_item, min(HEAD_ITEMS + (7 * (step + 1)) // 10, FIRST))
+            items = range(next_item, min(HEAD_ITEMS + (11 * (step + 1)) // 20, FIRST))
             next_item += len(items)
             for n in items:
                 regroup_w(n, 256)
+            for n in regrouped:
+                quantise_w(n)
+            regrouped = items
             if 2 <= step < PASSES + 2:
                 quantise_z(step - 2)
             if step == 8:
                 nc.sync.dma_start(out=b1b[:], in_=b1.partition_broadcast(P))
             if step >= 3:
-                multiply(wide, step - 3, w_codes.pop(step - 3), 0, N1)
+                codes = w_codes.pop(step - 3)
+                multiply(wide, step - 3, codes, 0, N1)
+                free_slots.append(codes)
             if step < PASSES:
                 transposes(step)
             target = min(TILES, LEAD_TILES + (8 * (step + 1)) // 5)
@@ -324,8 +354,6 @@ def tile_shiftedpatchtokenization_pa_kernel(tc, x, ln1_g, ln1_b, w1, b1, out):
                 for n in range(next_load, next_load + 3):
                     load_w(n)
                 next_load += 3
-            for n in items:
-                quantise_w(n)
         while next_load < ITEMS:
             load_w(next_load)
             next_load += 1
@@ -342,4 +370,5 @@ def tile_shiftedpatchtokenization_pa_kernel(tc, x, ln1_g, ln1_b, w1, b1, out):
                 codes = w_codes.pop(n - 1)
                 for h in range(2):
                     multiply(narrow, 2 * (n - 1 - FIRST) + h, codes, N2 * h, N2)
+                free_slots.append(codes)
         finish(narrow, N1, N2)

@@ -22,8 +22,8 @@ PASSES = 20
 N1, N2 = 512, 256
 ITEMS = 30
 FIRST = 20
-HEAD_ITEMS = 9
-SLOTS = 24
+HEAD_ITEMS = 6
+SLOTS = 22
 TILES = 32
 LEAD_TILES = 8
 
@@ -34,8 +34,8 @@ def tile_shiftedpatchtokenization_pa_kernel(tc, x, ln1_g, ln1_b, w1, b1, out):
         ctx.enter_context(tc.manual_schedule())
         consts = ctx.enter_context(tc.tile_pool(name="consts", bufs=1))
         wraw_pool = ctx.enter_context(tc.tile_pool(name="wraw", bufs=5))
-        wi_pool = ctx.enter_context(tc.tile_pool(name="wi", bufs=6))
-        xh_pool = ctx.enter_context(tc.tile_pool(name="xh", bufs=14))
+        wi_pool = ctx.enter_context(tc.tile_pool(name="wi", bufs=4))
+        xh_pool = ctx.enter_context(tc.tile_pool(name="xh", bufs=16))
         zp_pool = ctx.enter_context(tc.tile_pool(name="zp", bufs=2))
         zi_pool = ctx.enter_context(tc.tile_pool(name="zi", bufs=2))
         acc_pool = ctx.enter_context(tc.psum_pool(name="acc", bufs=1))
@@ -66,23 +66,15 @@ def tile_shiftedpatchtokenization_pa_kernel(tc, x, ln1_g, ln1_b, w1, b1, out):
         def regroup4(copy, dst, src):
             copy(out=dst.rearrange("p (c i) t -> p c t i", i=4), in_=src.rearrange("p t (c i) -> p c t i", i=4))
 
-        def regroup_w_head(n):
+        def regroup_w_gpsimd(n):
             wr = w_raw.pop(n)[:].rearrange("p (t n) -> p t n", t=4)
             wi = wi_pool.tile([P, 512, 4], BF16, name="wi", align_bytes=64)
-            for lo in range(0, 512, 256):
-                if n < 2:
-                    nc.gpsimd.tensor_scalar(
-                        out=wi[:, lo:lo + 256, :], in0=wr[:, :, lo:lo + 256].rearrange("p t n -> p n t"),
-                        scalar1=1.0, scalar2=0.0, op0=ALU.mult, op1=ALU.add,
-                    )
-                else:
-                    ps = tp_pool.tile([P, 256, 4], BF16, name="tp")
-                    for h in range(2):
-                        nc.tensor.matmul(
-                            out=ps[:, 128 * h:128 * h + 128, :].rearrange("p n t -> p (n t)"), lhsT=eye_bf[:],
-                            rhs=wr[:, :, lo + 128 * h:lo + 128 * h + 128].rearrange("p t n -> p n t"), start=True, stop=True,
-                        )
-                    nc.scalar.copy(out=wi[:, lo:lo + 256, :].rearrange("p n t -> p (n t)"), in_=ps[:].rearrange("p n t -> p (n t)"))
+            for lo in range(0, 512, 128):
+                nc.gpsimd.tensor_scalar(
+                    out=wi[:, lo:lo + 128, :].rearrange("p (c i) t -> p c t i", i=4),
+                    in0=wr[:, :, lo:lo + 128].rearrange("p t (c i) -> p c t i", i=4),
+                    scalar1=1.0, scalar2=0.0, op0=ALU.mult, op1=ALU.add,
+                )
             w_grouped[n] = wi
             load_w(n + 5)
 
@@ -114,20 +106,21 @@ def tile_shiftedpatchtokenization_pa_kernel(tc, x, ln1_g, ln1_b, w1, b1, out):
         nc.scalar.dma_start(out=gb[0:20, :], in_=ln1_g.rearrange("(r k) -> r k", k=512))
         nc.scalar.dma_start(out=gb[32:52, :], in_=ln1_b.rearrange("(r k) -> r k", k=512))
         xr = consts.tile([P, 4, 32, HW], BF16, name="xr")
-        for half in range(4):
-            for b in (half, half + 4):
-                nc.sync.dma_start(
-                    out=xr[b:b + 121:8, :, 8:24, :].rearrange("p c r w -> p c (r w)"),
-                    in_=x[b].rearrange("(c o) (i q) w -> (o i) c (q w)", o=2, i=8),
-                )
-        for n in range(5):
+        load_w(0)
+        for c in (0, 2):
+            for half in range(4):
+                for b in (half, half + 4):
+                    nc.sync.dma_start(
+                        out=xr[b:b + 121:8, c:c + 2, 8:24, :].rearrange("p c r w -> p c (r w)"),
+                        in_=x[b].rearrange("(c o) (i q) w -> (o i) c (q w)", o=2, i=8)[:, c:c + 2, :],
+                    )
+            load_w(1 + c // 2)
+        for n in range(3, 5):
             load_w(n)
         b1b = consts.tile([P, DIM], BF16, name="b1b")
 
         eye = consts.tile([P, P], F32, name="eye")
         make_identity(nc, eye[:])
-        eye_bf = consts.tile([P, P], BF16, name="eye_bf")
-        nc.vector.tensor_copy(out=eye_bf[:], in_=eye[:])
         perm = consts.tile([P, P], F32, name="perm")
         nc.vector.tensor_copy(
             out=perm[:].rearrange("p (o b i) -> p o b i", o=2, b=8), in_=eye[:].rearrange("p (o i b) -> p o b i", o=2, i=8)
@@ -153,13 +146,12 @@ def tile_shiftedpatchtokenization_pa_kernel(tc, x, ln1_g, ln1_b, w1, b1, out):
         nc.vector.memset(cells[:], 0.0)
         for a, rows in enumerate((upper, lower)):
             flat = rows[:].rearrange("p o m -> p (o m)")
-            nc.vector.tensor_scalar_mul(out=weights[:, 0, a, :], in0=flat, scalar1=128.0 / PD)
+            nc.vector.tensor_scalar_mul(out=weights[:, 0, a, :], in0=flat, scalar1=64.0 / PD)
             nc.vector.scalar_tensor_tensor(
-                out=weights[:, 1, a, :], in0=same[:].rearrange("p o m -> p (o m)"), scalar=128.0 / PD, in1=weights[:, 0, a, :], op0=ALU.mult, op1=ALU.add
+                out=weights[:, 1, a, :], in0=same[:].rearrange("p o m -> p (o m)"), scalar=64.0 / PD, in1=weights[:, 0, a, :], op0=ALU.mult, op1=ALU.add
             )
 
-        for n in range(2):
-            regroup_w_head(n)
+        regroup_w(0, 256)
 
         gk = consts.tile([P, 4, PASSES], F32, name="gk")
         bk = consts.tile([P, 4, PASSES], F32, name="bk")
@@ -171,10 +163,13 @@ def tile_shiftedpatchtokenization_pa_kernel(tc, x, ln1_g, ln1_b, w1, b1, out):
         nc.vector.tensor_copy(out=gk[:], in_=pt[:, :, 0:20])
         nc.vector.tensor_copy(out=bk[:], in_=pt[:, :, 32:52])
 
-        st6 = consts.tile([P, 2, 16, 6], F32, name="st6")
-        for a in range(2):
-            for j in range(16):
-                nc.vector.bn_stats(out=st6[:, a, j, :], in_=xr[:, :, 8 + 8 * a:16 + 8 * a, 8 * j:8 * j + 8])
+        quantise_w(0)
+        st6 = consts.tile([P, 2, 16, 2, 6], F32, name="st6")
+        for h in range(2):
+            for a in range(2):
+                for j in range(16):
+                    nc.vector.bn_stats(out=st6[:, a, j, h, :], in_=xr[:, 2 * h:2 * h + 2, 8 + 8 * a:16 + 8 * a, 8 * j:8 * j + 8])
+
         def neighbours(c, dst, rot, row):
             ps = tp_pool.tile([P, 1024], BF16, name="tp")
             rows = xr[:, c, row:row + 8, :].rearrange("p r w -> p (r w)")
@@ -185,19 +180,21 @@ def tile_shiftedpatchtokenization_pa_kernel(tc, x, ln1_g, ln1_b, w1, b1, out):
                 )
             nc.scalar.copy(out=xr[:, c, dst:dst + 8, :].rearrange("p r w -> p (r w)"), in_=ps[:])
 
+        regroup_w(1, 512)
         for c in range(4):
             neighbours(c, 0, rot_dn, 16)
-        for n in range(2, 5):
-            regroup_w_head(n)
-        groups = st6[:].rearrange("p a j (e k) -> p a j e k", e=2)
-        sqm = consts.tile([P, 2, 16, 2], F32, name="sqm")
+        regroup_w_gpsimd(2)
+        regroup_w_gpsimd(3)
+        regroup_w(4, 512)
+        groups = st6[:].rearrange("p a j h (e k) -> p a j (h e) k", e=2)
+        sqm = consts.tile([P, 2, 16, 4], F32, name="sqm")
         s2 = consts.tile([P, 2, 16], F32, name="s2")
         m2 = consts.tile([P, 2, 16], F32, name="m2")
         nc.vector.tensor_mul(out=sqm[:], in0=groups[:, :, :, :, 1], in1=groups[:, :, :, :, 1])
         nc.vector.tensor_reduce(out=m2[:], in_=groups[:, :, :, :, 2], axis=AX.X, op=ALU.add)
         nc.vector.tensor_reduce(out=s2[:], in_=sqm[:], axis=AX.X, op=ALU.add)
         nc.vector.tensor_reduce(out=cells[:, :, 0, 1:17], in_=groups[:, :, :, :, 1], axis=AX.X, op=ALU.add)
-        nc.vector.scalar_tensor_tensor(out=cells[:, :, 1, 1:17], in0=m2[:], scalar=1.0 / 128, in1=s2[:], op0=ALU.mult, op1=ALU.add)
+        nc.vector.scalar_tensor_tensor(out=cells[:, :, 1, 1:17], in0=m2[:], scalar=1.0 / 64, in1=s2[:], op0=ALU.mult, op1=ALU.add)
         columns = consts.tile([P, 2, 2, 2, 8], F32, name="columns")
         for a in range(2):
             nc.vector.tensor_add(out=columns[:, 0, a, :, :], in0=cells[:, a, :, 0:16:2], in1=cells[:, a, :, 3:18:2])
@@ -211,8 +208,8 @@ def tile_shiftedpatchtokenization_pa_kernel(tc, x, ln1_g, ln1_b, w1, b1, out):
                 start=(n == 0),
                 stop=(n == 3),
             )
-        quantise_w(0)
         quantise_w(1)
+        regroup_w(5, 512)
         tot = consts.tile([P, 2, 8], F32, name="tot")
         small = {}
         for nm in ("msq", "var", "r0", "nt", "rstd", "nmr"):
@@ -300,8 +297,8 @@ def tile_shiftedpatchtokenization_pa_kernel(tc, x, ln1_g, ln1_b, w1, b1, out):
 
         out_rows = out.rearrange("b (i j) n -> j (b i) n", j=8)
 
-        def finish(acc, first, width):
-            for tt in range(4):
+        def finish(acc, first, width, tts):
+            for tt in tts:
                 o = wraw_pool.tile([P, N1], F32, name="wr")
                 nc.vector.tensor_tensor(out=o[:, 0:width], in0=acc[tt][:, 0:width], in1=b1b[:, first:first + width], op=ALU.add)
                 for jl in range(2):
@@ -311,13 +308,9 @@ def tile_shiftedpatchtokenization_pa_kernel(tc, x, ln1_g, ln1_b, w1, b1, out):
         for tt in range(4):
             wide[tt] = acc_pool.tile([P, N1], F32, name="acc%d" % tt)
         for k in range(LEAD_TILES):
-            if k == 4:
-                for n in range(5, HEAD_ITEMS):
-                    quantise_w(n - 3)
-                    regroup_w_head(n)
-            normalise(k, 2 if k < 4 else 0)
+            normalise(k, 2 if k < 4 else 1)
         made = LEAD_TILES
-        for n in range(HEAD_ITEMS - 3, HEAD_ITEMS):
+        for n in range(2, HEAD_ITEMS):
             quantise_w(n)
         next_item = HEAD_ITEMS
         regrouped = []
@@ -329,10 +322,10 @@ def tile_shiftedpatchtokenization_pa_kernel(tc, x, ln1_g, ln1_b, w1, b1, out):
                 neighbours(step - 1, 24, rot_up, 8)
             if 2 <= step < PASSES + 2:
                 regroup_z(step - 2)
-            items = range(next_item, min(HEAD_ITEMS + (11 * (step + 1)) // 20, FIRST))
+            items = range(next_item, min(HEAD_ITEMS + (13 * (step + 1)) // 20, FIRST))
             next_item += len(items)
             for n in items:
-                regroup_w(n, 256)
+                regroup_w(n, 192)
             for n in regrouped:
                 quantise_w(n)
             regrouped = items
@@ -362,13 +355,13 @@ def tile_shiftedpatchtokenization_pa_kernel(tc, x, ln1_g, ln1_b, w1, b1, out):
             narrow[tt] = tp_pool.tile([P, N2], F32, name="tp")
         for n in range(FIRST, ITEMS + 1):
             if n < ITEMS:
-                regroup_w(n, 256)
-            if n == FIRST + 1:
-                finish(wide, 0, N1)
+                regroup_w(n, 288)
             if n > FIRST:
                 quantise_w(n - 1)
                 codes = w_codes.pop(n - 1)
                 for h in range(2):
                     multiply(narrow, 2 * (n - 1 - FIRST) + h, codes, N2 * h, N2)
                 free_slots.append(codes)
-        finish(narrow, N1, N2)
+            if FIRST <= n < FIRST + 4:
+                finish(wide, 0, N1, (n - FIRST,))
+        finish(narrow, N1, N2, range(4))

@@ -64,7 +64,7 @@ def tile_shiftedpatchtokenization_pa_kernel(tc, x, ln1_g, ln1_b, w1, b1, out):
             w_raw[n] = wr
 
         def regroup4(copy, dst, src):
-            copy(out=dst.rearrange("p (c i) t -> p c t i", i=4), in_=src.rearrange("p t (c i) -> p c t i", i=4))
+            copy(out=dst.rearrange("p (c i) t -> p c t i", i=8), in_=src.rearrange("p t (c i) -> p c t i", i=8))
 
         def regroup_w_gpsimd(n):
             wr = w_raw.pop(n)[:].rearrange("p (t n) -> p t n", t=4)

@@ -22,7 +22,7 @@ PASSES = 20
 N1, N2 = 512, 256
 ITEMS = 30
 FIRST = 20
-HEAD_ITEMS = 6
+HEAD_ITEMS = 7
 SLOTS = 22
 TILES = 32
 LEAD_TILES = 8
@@ -34,7 +34,7 @@ def tile_shiftedpatchtokenization_pa_kernel(tc, x, ln1_g, ln1_b, w1, b1, out):
         ctx.enter_context(tc.manual_schedule())
         consts = ctx.enter_context(tc.tile_pool(name="consts", bufs=1))
         wraw_pool = ctx.enter_context(tc.tile_pool(name="wraw", bufs=5))
-        wi_pool = ctx.enter_context(tc.tile_pool(name="wi", bufs=4))
+        wi_pool = ctx.enter_context(tc.tile_pool(name="wi", bufs=5))
         xh_pool = ctx.enter_context(tc.tile_pool(name="xh", bufs=16))
         zp_pool = ctx.enter_context(tc.tile_pool(name="zp", bufs=2))
         zi_pool = ctx.enter_context(tc.tile_pool(name="zi", bufs=2))
@@ -114,24 +114,27 @@ def tile_shiftedpatchtokenization_pa_kernel(tc, x, ln1_g, ln1_b, w1, b1, out):
                         out=xr[b:b + 121:8, c:c + 2, 8:24, :].rearrange("p c r w -> p c (r w)"),
                         in_=x[b].rearrange("(c o) (i q) w -> (o i) c (q w)", o=2, i=8)[:, c:c + 2, :],
                     )
-            load_w(1 + c // 2)
-        for n in range(3, 5):
+        for n in range(1, 5):
             load_w(n)
         b1b = consts.tile([P, DIM], BF16, name="b1b")
 
         eye = consts.tile([P, P], F32, name="eye")
         make_identity(nc, eye[:])
+        nc.gpsimd.memset(xr[:, :, 24:32, :], 0.0)
+        for o in range(2):
+            for c in range(4):
+                nc.sync.dma_start(
+                    out=xr[64 * o:64 * o + 56, c, 24:32, :].rearrange("p r w -> p (r w)"),
+                    in_=x[:, 2 * c + o, :, :].rearrange("b (i q) w -> i b (q w)", q=16)[1:8, :, 0:1024],
+                )
         perm = consts.tile([P, P], F32, name="perm")
         nc.vector.tensor_copy(
             out=perm[:].rearrange("p (o b i) -> p o b i", o=2, b=8), in_=eye[:].rearrange("p (o i b) -> p o b i", o=2, i=8)
         )
         rot_dn = consts.tile([P, 2, 64], BF16, name="rot_dn")
-        rot_up = consts.tile([P, 2, 64], BF16, name="rot_up")
         nc.vector.memset(rot_dn[:], 0.0)
-        nc.vector.memset(rot_up[:], 0.0)
         eye2 = eye[:].rearrange("p (o m) -> p o m", o=2)
         nc.vector.tensor_copy(out=rot_dn[:, :, 8:64], in_=eye2[:, :, 0:56])
-        nc.vector.tensor_copy(out=rot_up[:, :, 0:56], in_=eye2[:, :, 8:64])
         same = consts.tile([P, 2, 64], F32, name="same")
         upper = consts.tile([P, 2, 64], F32, name="upper")
         lower = consts.tile([P, 2, 64], F32, name="lower")
@@ -186,6 +189,7 @@ def tile_shiftedpatchtokenization_pa_kernel(tc, x, ln1_g, ln1_b, w1, b1, out):
         regroup_w_gpsimd(2)
         regroup_w_gpsimd(3)
         regroup_w(4, 512)
+        regroup_w(5, 512)
         groups = st6[:].rearrange("p a j h (e k) -> p a j (h e) k", e=2)
         sqm = consts.tile([P, 2, 16, 4], F32, name="sqm")
         s2 = consts.tile([P, 2, 16], F32, name="s2")
@@ -209,7 +213,6 @@ def tile_shiftedpatchtokenization_pa_kernel(tc, x, ln1_g, ln1_b, w1, b1, out):
                 stop=(n == 3),
             )
         quantise_w(1)
-        regroup_w(5, 512)
         tot = consts.tile([P, 2, 8], F32, name="tot")
         small = {}
         for nm in ("msq", "var", "r0", "nt", "rstd", "nmr"):
@@ -220,6 +223,8 @@ def tile_shiftedpatchtokenization_pa_kernel(tc, x, ln1_g, ln1_b, w1, b1, out):
         nc.vector.scalar_tensor_tensor(out=var[:], in0=tot[:, 1, :], scalar=EPS, in1=msq[:], op0=ALU.add, op1=ALU.subtract)
         nc.vector.tensor_scalar_max(out=var[:], in0=var[:], scalar1=EPS)
         nc.scalar.activation(out=r0[:], in_=var[:], func=ACT.Abs_reciprocal_sqrt)
+        quantise_w(2)
+        regroup_w(6, 512)
         nc.vector.scalar_tensor_tensor(out=nt[:], in0=r0[:], scalar=-0.5, in1=r0[:], op0=ALU.mult, op1=ALU.mult)
         nc.vector.tensor_mul(out=nt[:], in0=nt[:], in1=var[:])
         nc.vector.scalar_tensor_tensor(out=rstd[:], in0=nt[:], scalar=1.5, in1=r0[:], op0=ALU.add, op1=ALU.mult)
@@ -310,7 +315,7 @@ def tile_shiftedpatchtokenization_pa_kernel(tc, x, ln1_g, ln1_b, w1, b1, out):
         for k in range(LEAD_TILES):
             normalise(k, 2 if k < 4 else 1)
         made = LEAD_TILES
-        for n in range(2, HEAD_ITEMS):
+        for n in range(3, HEAD_ITEMS):
             quantise_w(n)
         next_item = HEAD_ITEMS
         regrouped = []
@@ -318,14 +323,12 @@ def tile_shiftedpatchtokenization_pa_kernel(tc, x, ln1_g, ln1_b, w1, b1, out):
         for step in range(PASSES + 3):
             if 1 <= step < PASSES + 1:
                 evacuate(step - 1)
-            if 1 <= step < 5:
-                neighbours(step - 1, 24, rot_up, 8)
             if 2 <= step < PASSES + 2:
                 regroup_z(step - 2)
             items = range(next_item, min(HEAD_ITEMS + (13 * (step + 1)) // 20, FIRST))
             next_item += len(items)
             for n in items:
-                regroup_w(n, 192)
+                regroup_w(n, 208)
             for n in regrouped:
                 quantise_w(n)
             regrouped = items
@@ -355,7 +358,7 @@ def tile_shiftedpatchtokenization_pa_kernel(tc, x, ln1_g, ln1_b, w1, b1, out):
             narrow[tt] = tp_pool.tile([P, N2], F32, name="tp")
         for n in range(FIRST, ITEMS + 1):
             if n < ITEMS:
-                regroup_w(n, 288)
+                regroup_w(n, 320)
             if n > FIRST:
                 quantise_w(n - 1)
                 codes = w_codes.pop(n - 1)

@@ -121,12 +121,6 @@ def tile_shiftedpatchtokenization_pa_kernel(tc, x, ln1_g, ln1_b, w1, b1, out):
         eye = consts.tile([P, P], F32, name="eye")
         make_identity(nc, eye[:])
         nc.gpsimd.memset(xr[:, :, 24:32, :], 0.0)
-        for o in range(2):
-            for c in range(4):
-                nc.sync.dma_start(
-                    out=xr[64 * o:64 * o + 56, c, 24:32, :].rearrange("p r w -> p (r w)"),
-                    in_=x[:, 2 * c + o, :, :].rearrange("b (i q) w -> i b (q w)", q=16)[1:8, :, 0:1024],
-                )
         perm = consts.tile([P, P], F32, name="perm")
         nc.vector.tensor_copy(
             out=perm[:].rearrange("p (o b i) -> p o b i", o=2, b=8), in_=eye[:].rearrange("p (o i b) -> p o b i", o=2, i=8)
@@ -320,6 +314,12 @@ def tile_shiftedpatchtokenization_pa_kernel(tc, x, ln1_g, ln1_b, w1, b1, out):
         next_item = HEAD_ITEMS
         regrouped = []
         next_load = FIRST
+        for o in range(2):
+            for c in range(4):
+                nc.sync.dma_start(
+                    out=xr[64 * o:64 * o + 56, c, 24:32, :].rearrange("p r w -> p (r w)"),
+                    in_=x[:, 2 * c + o, :, :].rearrange("b (i q) w -> i b (q w)", q=16)[1:8, :, 0:1024],
+                )
         for step in range(PASSES + 3):
             if 1 <= step < PASSES + 1:
                 evacuate(step - 1)

@@ -71,8 +71,7 @@ def tile_shiftedpatchtokenization_pa_kernel(tc, x, ln1_g, ln1_b, w1, b1, out):
             wi = wi_pool.tile([P, 512, 4], BF16, name="wi", align_bytes=64)
             for lo in range(0, 512, 128):
                 nc.gpsimd.tensor_scalar(
-                    out=wi[:, lo:lo + 128, :].rearrange("p (c i) t -> p c t i", i=4),
-                    in0=wr[:, :, lo:lo + 128].rearrange("p t (c i) -> p c t i", i=4),
+                    out=wi[:, lo:lo + 128, :], in0=wr[:, :, lo:lo + 128].rearrange("p t n -> p n t"),
                     scalar1=1.0, scalar2=0.0, op0=ALU.mult, op1=ALU.add,
                 )
             w_grouped[n] = wi

@@ -22,7 +22,12 @@ PASSES = 20
 N1, N2 = 512, 256
 ITEMS = 30
 FIRST = 20
-HEAD_ITEMS = 7
+TEN = (6, 7, 8)
+A, B_ = 1, 2
+W1, W2, W3 = 3, 1, 14
+SH1 = 208
+SH2 = 320
+HEAD_ITEMS = 9
 SLOTS = 22
 TILES = 32
 LEAD_TILES = 8
@@ -77,6 +82,22 @@ def tile_shiftedpatchtokenization_pa_kernel(tc, x, ln1_g, ln1_b, w1, b1, out):
             w_grouped[n] = wi
             load_w(n + 5)
 
+        def regroup_w_tensor(n):
+            wr = w_raw.pop(n)[:].rearrange("p (t n) -> p t n", t=4)
+            wi = wi_pool.tile([P, 512, 4], BF16, name="wi", align_bytes=64)
+            for half in range(2):
+                ps = acc_pool.tile([P, 1024], BF16, name="acc%d" % (2 * (n % 2) + half))
+                for h in range(2):
+                    lo = 256 * half + 128 * h
+                    nc.tensor.matmul(
+                        out=ps[:, 512 * h:512 * h + 512], lhsT=eye_bf[:], rhs=wr[:, :, lo:lo + 128].rearrange("p t n -> p n t"),
+                        start=True, stop=True,
+                    )
+                nc.scalar.copy(out=wi[:, 256 * half:256 * half + 256, :].rearrange("p n t -> p (n t)"), in_=ps[:])
+            w_grouped[n] = wi
+            if n + 5 < FIRST:
+                load_w(n + 5)
+
         def regroup_w(n, scalar_cols):
             wr = w_raw.pop(n)
             wi = wi_pool.tile([P, 512, 4], BF16, name="wi", align_bytes=64)
@@ -119,6 +140,8 @@ def tile_shiftedpatchtokenization_pa_kernel(tc, x, ln1_g, ln1_b, w1, b1, out):
 
         eye = consts.tile([P, P], F32, name="eye")
         make_identity(nc, eye[:])
+        eye_bf = consts.tile([P, P], BF16, name="eye_bf")
+        nc.vector.tensor_copy(out=eye_bf[:], in_=eye[:])
         nc.gpsimd.memset(xr[:, :, 24:32, :], 0.0)
         perm = consts.tile([P, P], F32, name="perm")
         nc.vector.tensor_copy(
@@ -149,19 +172,9 @@ def tile_shiftedpatchtokenization_pa_kernel(tc, x, ln1_g, ln1_b, w1, b1, out):
 
         regroup_w(0, 256)
 
-        gk = consts.tile([P, 4, PASSES], F32, name="gk")
-        bk = consts.tile([P, 4, PASSES], F32, name="bk")
-        gb_t = consts.tile([P, 4, P], F32, name="gb_t")
-        nc.vector.tensor_copy(out=gb_t[:], in_=gb[:].rearrange("r (p t) -> r t p", t=4))
-        pt = tp_pool.tile([P, 4, P], F32, name="tp")
-        for t in range(4):
-            nc.tensor.transpose(out=pt[:, t, :], in_=gb_t[:, t, :], identity=eye[:])
-        nc.vector.tensor_copy(out=gk[:], in_=pt[:, :, 0:20])
-        nc.vector.tensor_copy(out=bk[:], in_=pt[:, :, 32:52])
-
-        quantise_w(0)
         st6 = consts.tile([P, 2, 16, 2, 6], F32, name="st6")
-        for h in range(2):
+
+        def cell_stats(h):
             for a in range(2):
                 for j in range(16):
                     nc.vector.bn_stats(out=st6[:, a, j, h, :], in_=xr[:, 2 * h:2 * h + 2, 8 + 8 * a:16 + 8 * a, 8 * j:8 * j + 8])
@@ -176,13 +189,27 @@ def tile_shiftedpatchtokenization_pa_kernel(tc, x, ln1_g, ln1_b, w1, b1, out):
                 )
             nc.scalar.copy(out=xr[:, c, dst:dst + 8, :].rearrange("p r w -> p (r w)"), in_=ps[:])
 
-        regroup_w(1, 512)
-        for c in range(4):
+        cell_stats(0)
+        for c in range(2):
             neighbours(c, 0, rot_dn, 16)
+        gk = consts.tile([P, 4, PASSES], F32, name="gk")
+        bk = consts.tile([P, 4, PASSES], F32, name="bk")
+        gb_t = consts.tile([P, 4, P], F32, name="gb_t")
+        nc.vector.tensor_copy(out=gb_t[:], in_=gb[:].rearrange("r (p t) -> r t p", t=4))
+        quantise_w(0)
+        regroup_w(1, 512)
+        cell_stats(1)
+        for c in range(2, 4):
+            neighbours(c, 0, rot_dn, 16)
+        pt = tp_pool.tile([P, 4, P], F32, name="tp")
+        for t in range(4):
+            nc.tensor.transpose(out=pt[:, t, :], in_=gb_t[:, t, :], identity=eye[:])
         regroup_w_gpsimd(2)
         regroup_w_gpsimd(3)
         regroup_w(4, 512)
         regroup_w(5, 512)
+        for n in TEN[0:A]:
+            regroup_w_tensor(n)
         groups = st6[:].rearrange("p a j h (e k) -> p a j (h e) k", e=2)
         sqm = consts.tile([P, 2, 16, 4], F32, name="sqm")
         s2 = consts.tile([P, 2, 16], F32, name="s2")
@@ -193,9 +220,8 @@ def tile_shiftedpatchtokenization_pa_kernel(tc, x, ln1_g, ln1_b, w1, b1, out):
         nc.vector.tensor_reduce(out=cells[:, :, 0, 1:17], in_=groups[:, :, :, :, 1], axis=AX.X, op=ALU.add)
         nc.vector.scalar_tensor_tensor(out=cells[:, :, 1, 1:17], in0=m2[:], scalar=1.0 / 64, in1=s2[:], op0=ALU.mult, op1=ALU.add)
         columns = consts.tile([P, 2, 2, 2, 8], F32, name="columns")
-        for a in range(2):
-            nc.vector.tensor_add(out=columns[:, 0, a, :, :], in0=cells[:, a, :, 0:16:2], in1=cells[:, a, :, 3:18:2])
-            nc.vector.tensor_add(out=columns[:, 1, a, :, :], in0=cells[:, a, :, 1:17:2], in1=cells[:, a, :, 2:18:2])
+        nc.vector.tensor_add(out=columns[:, 0, :, :, :], in0=cells[:, :, :, 0:16:2], in1=cells[:, :, :, 3:18:2])
+        nc.vector.tensor_add(out=columns[:, 1, :, :, :], in0=cells[:, :, :, 1:17:2], in1=cells[:, :, :, 2:18:2])
         st = tp_pool.tile([P, 2, 8], F32, name="tp")
         for n in range(4):
             nc.tensor.matmul(
@@ -205,6 +231,9 @@ def tile_shiftedpatchtokenization_pa_kernel(tc, x, ln1_g, ln1_b, w1, b1, out):
                 start=(n == 0),
                 stop=(n == 3),
             )
+        nc.vector.tensor_copy(out=gk[:], in_=pt[:, :, 0:20])
+        nc.vector.tensor_copy(out=bk[:], in_=pt[:, :, 32:52])
+
         quantise_w(1)
         tot = consts.tile([P, 2, 8], F32, name="tot")
         small = {}
@@ -217,7 +246,8 @@ def tile_shiftedpatchtokenization_pa_kernel(tc, x, ln1_g, ln1_b, w1, b1, out):
         nc.vector.tensor_scalar_max(out=var[:], in0=var[:], scalar1=EPS)
         nc.scalar.activation(out=r0[:], in_=var[:], func=ACT.Abs_reciprocal_sqrt)
         quantise_w(2)
-        regroup_w(6, 512)
+        for n in TEN[A:B_]:
+            regroup_w_tensor(n)
         nc.vector.scalar_tensor_tensor(out=nt[:], in0=r0[:], scalar=-0.5, in1=r0[:], op0=ALU.mult, op1=ALU.mult)
         nc.vector.tensor_mul(out=nt[:], in0=nt[:], in1=var[:])
         nc.vector.scalar_tensor_tensor(out=rstd[:], in0=nt[:], scalar=1.5, in1=r0[:], op0=ALU.add, op1=ALU.mult)
@@ -307,6 +337,9 @@ def tile_shiftedpatchtokenization_pa_kernel(tc, x, ln1_g, ln1_b, w1, b1, out):
             wide[tt] = acc_pool.tile([P, N1], F32, name="acc%d" % tt)
         for k in range(LEAD_TILES):
             normalise(k, 2 if k < 4 else 1)
+            if k == 3:
+                for n in TEN[B_:]:
+                    regroup_w_tensor(n)
         made = LEAD_TILES
         for n in range(3, HEAD_ITEMS):
             quantise_w(n)
@@ -324,10 +357,10 @@ def tile_shiftedpatchtokenization_pa_kernel(tc, x, ln1_g, ln1_b, w1, b1, out):
                 evacuate(step - 1)
             if 2 <= step < PASSES + 2:
                 regroup_z(step - 2)
-            items = range(next_item, min(HEAD_ITEMS + (13 * (step + 1)) // 20, FIRST))
+            items = range(next_item, min(HEAD_ITEMS + (step + 1) // W1 + W2 * max(0, step - W3), FIRST))
             next_item += len(items)
             for n in items:
-                regroup_w(n, 208)
+                regroup_w(n, 240 if step < 15 else 192)
             for n in regrouped:
                 quantise_w(n)
             regrouped = items
@@ -357,7 +390,7 @@ def tile_shiftedpatchtokenization_pa_kernel(tc, x, ln1_g, ln1_b, w1, b1, out):
             narrow[tt] = tp_pool.tile([P, N2], F32, name="tp")
         for n in range(FIRST, ITEMS + 1):
             if n < ITEMS:
-                regroup_w(n, 320)
+                regroup_w(n, SH2)
             if n > FIRST:
                 quantise_w(n - 1)
                 codes = w_codes.pop(n - 1)

@@ -22,12 +22,7 @@ PASSES = 20
 N1, N2 = 512, 256
 ITEMS = 30
 FIRST = 20
-TEN = (6, 7, 8)
-A, B_ = 1, 2
-W1, W2, W3 = 3, 1, 14
-SH1 = 208
-SH2 = 320
-HEAD_ITEMS = 9
+HEAD_ITEMS = 7
 SLOTS = 22
 TILES = 32
 LEAD_TILES = 8
@@ -82,22 +77,6 @@ def tile_shiftedpatchtokenization_pa_kernel(tc, x, ln1_g, ln1_b, w1, b1, out):
             w_grouped[n] = wi
             load_w(n + 5)
 
-        def regroup_w_tensor(n):
-            wr = w_raw.pop(n)[:].rearrange("p (t n) -> p t n", t=4)
-            wi = wi_pool.tile([P, 512, 4], BF16, name="wi", align_bytes=64)
-            for half in range(2):
-                ps = acc_pool.tile([P, 1024], BF16, name="acc%d" % (2 * (n % 2) + half))
-                for h in range(2):
-                    lo = 256 * half + 128 * h
-                    nc.tensor.matmul(
-                        out=ps[:, 512 * h:512 * h + 512], lhsT=eye_bf[:], rhs=wr[:, :, lo:lo + 128].rearrange("p t n -> p n t"),
-                        start=True, stop=True,
-                    )
-                nc.scalar.copy(out=wi[:, 256 * half:256 * half + 256, :].rearrange("p n t -> p (n t)"), in_=ps[:])
-            w_grouped[n] = wi
-            if n + 5 < FIRST:
-                load_w(n + 5)
-
         def regroup_w(n, scalar_cols):
             wr = w_raw.pop(n)
             wi = wi_pool.tile([P, 512, 4], BF16, name="wi", align_bytes=64)
@@ -140,8 +119,6 @@ def tile_shiftedpatchtokenization_pa_kernel(tc, x, ln1_g, ln1_b, w1, b1, out):
 
         eye = consts.tile([P, P], F32, name="eye")
         make_identity(nc, eye[:])
-        eye_bf = consts.tile([P, P], BF16, name="eye_bf")
-        nc.vector.tensor_copy(out=eye_bf[:], in_=eye[:])
         nc.gpsimd.memset(xr[:, :, 24:32, :], 0.0)
         perm = consts.tile([P, P], F32, name="perm")
         nc.vector.tensor_copy(
@@ -208,8 +185,6 @@ def tile_shiftedpatchtokenization_pa_kernel(tc, x, ln1_g, ln1_b, w1, b1, out):
         regroup_w_gpsimd(3)
         regroup_w(4, 512)
         regroup_w(5, 512)
-        for n in TEN[0:A]:
-            regroup_w_tensor(n)
         groups = st6[:].rearrange("p a j h (e k) -> p a j (h e) k", e=2)
         sqm = consts.tile([P, 2, 16, 4], F32, name="sqm")
         s2 = consts.tile([P, 2, 16], F32, name="s2")
@@ -246,8 +221,7 @@ def tile_shiftedpatchtokenization_pa_kernel(tc, x, ln1_g, ln1_b, w1, b1, out):
         nc.vector.tensor_scalar_max(out=var[:], in0=var[:], scalar1=EPS)
         nc.scalar.activation(out=r0[:], in_=var[:], func=ACT.Abs_reciprocal_sqrt)
         quantise_w(2)
-        for n in TEN[A:B_]:
-            regroup_w_tensor(n)
+        regroup_w(6, 512)
         nc.vector.scalar_tensor_tensor(out=nt[:], in0=r0[:], scalar=-0.5, in1=r0[:], op0=ALU.mult, op1=ALU.mult)
         nc.vector.tensor_mul(out=nt[:], in0=nt[:], in1=var[:])
         nc.vector.scalar_tensor_tensor(out=rstd[:], in0=nt[:], scalar=1.5, in1=r0[:], op0=ALU.add, op1=ALU.mult)
@@ -337,9 +311,6 @@ def tile_shiftedpatchtokenization_pa_kernel(tc, x, ln1_g, ln1_b, w1, b1, out):
             wide[tt] = acc_pool.tile([P, N1], F32, name="acc%d" % tt)
         for k in range(LEAD_TILES):
             normalise(k, 2 if k < 4 else 1)
-            if k == 3:
-                for n in TEN[B_:]:
-                    regroup_w_tensor(n)
         made = LEAD_TILES
         for n in range(3, HEAD_ITEMS):
             quantise_w(n)
@@ -357,10 +328,10 @@ def tile_shiftedpatchtokenization_pa_kernel(tc, x, ln1_g, ln1_b, w1, b1, out):
                 evacuate(step - 1)
             if 2 <= step < PASSES + 2:
                 regroup_z(step - 2)
-            items = range(next_item, min(HEAD_ITEMS + (step + 1) // W1 + W2 * max(0, step - W3), FIRST))
+            items = range(next_item, min(HEAD_ITEMS + (step + 1) // 2 + max(0, step - 15), FIRST))
             next_item += len(items)
             for n in items:
-                regroup_w(n, 240 if step < 15 else 192)
+                regroup_w(n, 208)
             for n in regrouped:
                 quantise_w(n)
             regrouped = items
@@ -390,7 +361,7 @@ def tile_shiftedpatchtokenization_pa_kernel(tc, x, ln1_g, ln1_b, w1, b1, out):
             narrow[tt] = tp_pool.tile([P, N2], F32, name="tp")
         for n in range(FIRST, ITEMS + 1):
             if n < ITEMS:
-                regroup_w(n, SH2)
+                regroup_w(n, 352 if n < FIRST + 4 else 304)
             if n > FIRST:
                 quantise_w(n - 1)
                 codes = w_codes.pop(n - 1)

@@ -35,7 +35,7 @@ def tile_shiftedpatchtokenization_pa_kernel(tc, x, ln1_g, ln1_b, w1, b1, out):
         consts = ctx.enter_context(tc.tile_pool(name="consts", bufs=1))
         wraw_pool = ctx.enter_context(tc.tile_pool(name="wraw", bufs=5))
         wi_pool = ctx.enter_context(tc.tile_pool(name="wi", bufs=5))
-        xh_pool = ctx.enter_context(tc.tile_pool(name="xh", bufs=16))
+        xh_pool = ctx.enter_context(tc.tile_pool(name="xh", bufs=12))
         zp_pool = ctx.enter_context(tc.tile_pool(name="zp", bufs=2))
         zi_pool = ctx.enter_context(tc.tile_pool(name="zi", bufs=2))
         acc_pool = ctx.enter_context(tc.psum_pool(name="acc", bufs=1))
@@ -169,22 +169,13 @@ def tile_shiftedpatchtokenization_pa_kernel(tc, x, ln1_g, ln1_b, w1, b1, out):
         cell_stats(0)
         for c in range(2):
             neighbours(c, 0, rot_dn, 16)
-        gk = consts.tile([P, 4, PASSES], F32, name="gk")
-        bk = consts.tile([P, 4, PASSES], F32, name="bk")
-        gb_t = consts.tile([P, 4, P], F32, name="gb_t")
-        nc.vector.tensor_copy(out=gb_t[:], in_=gb[:].rearrange("r (p t) -> r t p", t=4))
-        quantise_w(0)
-        regroup_w(1, 512)
         cell_stats(1)
         for c in range(2, 4):
             neighbours(c, 0, rot_dn, 16)
-        pt = tp_pool.tile([P, 4, P], F32, name="tp")
-        for t in range(4):
-            nc.tensor.transpose(out=pt[:, t, :], in_=gb_t[:, t, :], identity=eye[:])
+        regroup_w_gpsimd(1)
         regroup_w_gpsimd(2)
-        regroup_w_gpsimd(3)
-        regroup_w(4, 512)
-        regroup_w(5, 512)
+        for n in (3, 4, 5):
+            regroup_w(n, 512)
         groups = st6[:].rearrange("p a j h (e k) -> p a j (h e) k", e=2)
         sqm = consts.tile([P, 2, 16, 4], F32, name="sqm")
         s2 = consts.tile([P, 2, 16], F32, name="s2")
@@ -206,10 +197,15 @@ def tile_shiftedpatchtokenization_pa_kernel(tc, x, ln1_g, ln1_b, w1, b1, out):
                 start=(n == 0),
                 stop=(n == 3),
             )
-        nc.vector.tensor_copy(out=gk[:], in_=pt[:, :, 0:20])
-        nc.vector.tensor_copy(out=bk[:], in_=pt[:, :, 32:52])
+        gk = consts.tile([P, 4, PASSES], F32, name="gk")
+        bk = consts.tile([P, 4, PASSES], F32, name="bk")
+        gb_t = consts.tile([P, 4, P], F32, name="gb_t")
+        nc.vector.tensor_copy(out=gb_t[:], in_=gb[:].rearrange("r (p t) -> r t p", t=4))
+        pt = tp_pool.tile([P, 4, P], F32, name="tp")
+        for t in range(4):
+            nc.tensor.transpose(out=pt[:, t, :], in_=gb_t[:, t, :], identity=eye[:])
 
-        quantise_w(1)
+        quantise_w(0)
         tot = consts.tile([P, 2, 8], F32, name="tot")
         small = {}
         for nm in ("msq", "var", "r0", "nt", "rstd", "nmr"):
@@ -220,12 +216,15 @@ def tile_shiftedpatchtokenization_pa_kernel(tc, x, ln1_g, ln1_b, w1, b1, out):
         nc.vector.scalar_tensor_tensor(out=var[:], in0=tot[:, 1, :], scalar=EPS, in1=msq[:], op0=ALU.add, op1=ALU.subtract)
         nc.vector.tensor_scalar_max(out=var[:], in0=var[:], scalar1=EPS)
         nc.scalar.activation(out=r0[:], in_=var[:], func=ACT.Abs_reciprocal_sqrt)
-        quantise_w(2)
+        quantise_w(1)
         regroup_w(6, 512)
         nc.vector.scalar_tensor_tensor(out=nt[:], in0=r0[:], scalar=-0.5, in1=r0[:], op0=ALU.mult, op1=ALU.mult)
         nc.vector.tensor_mul(out=nt[:], in0=nt[:], in1=var[:])
         nc.vector.scalar_tensor_tensor(out=rstd[:], in0=nt[:], scalar=1.5, in1=r0[:], op0=ALU.add, op1=ALU.mult)
         nc.vector.scalar_tensor_tensor(out=nmr[:], in0=tot[:, 0, :], scalar=-1.0, in1=rstd[:], op0=ALU.mult, op1=ALU.mult)
+
+        nc.vector.tensor_copy(out=gk[:], in_=pt[:, :, 0:20])
+        nc.vector.tensor_copy(out=bk[:], in_=pt[:, :, 32:52])
 
         def affine(on_scalar, dst, src, scale, bias):
             if on_scalar:
@@ -234,11 +233,12 @@ def tile_shiftedpatchtokenization_pa_kernel(tc, x, ln1_g, ln1_b, w1, b1, out):
                 nc.vector.tensor_scalar(out=dst, in0=src, scalar1=scale, scalar2=bias, op0=ALU.mult, op1=ALU.add)
 
         xh_tiles = {}
+        edge_tiles = {(j, n): consts.tile([P, 1280], F32, name="edge%d%d" % (j, n)) for j in (0, 7) for n in range(2)}
 
         def normalise(k, n_scalar):
             j = k % 8
             row0 = 8 + 4 * (k // 8)
-            xh = xh_pool.tile([P, 1280], F32, name="xh")
+            xh = edge_tiles[j, (k // 8) % 2] if j in (0, 7) else xh_pool.tile([P, 1280], F32, name="xh")
             view = xh[:].rearrange("p (q e s c) -> p q e s c", q=4, e=16, s=5)
             for s, (di, dj) in enumerate(SHIFTS):
                 col0 = 16 * j + 8 * dj
@@ -247,7 +247,7 @@ def tile_shiftedpatchtokenization_pa_kernel(tc, x, ln1_g, ln1_b, w1, b1, out):
                 on_scalar = s >= 5 - n_scalar
                 src = xr[:, :, row0 + 8 * di:row0 + 8 * di + 4, col0 + lo:col0 + hi].rearrange("p c q e -> p q e c")
                 affine(on_scalar, view[:, :, lo:hi, s, :], src, rstd[:, j:j + 1], nmr[:, j:j + 1])
-                if hi - lo < 16:
+                if hi - lo < 16 and k < 16:
                     affine(on_scalar, view[:, :, 8 - lo:24 - hi, s, :], src, 0.0, nmr[:, j:j + 1])
             xh_tiles[k] = xh
 
@@ -312,7 +312,7 @@ def tile_shiftedpatchtokenization_pa_kernel(tc, x, ln1_g, ln1_b, w1, b1, out):
         for k in range(LEAD_TILES):
             normalise(k, 2 if k < 4 else 1)
         made = LEAD_TILES
-        for n in range(3, HEAD_ITEMS):
+        for n in range(2, HEAD_ITEMS):
             quantise_w(n)
         next_item = HEAD_ITEMS
         regrouped = []

@@ -283,10 +283,10 @@ def tile_shiftedpatchtokenization_pa_kernel(tc, x, ln1_g, ln1_b, w1, b1, out):
             nc.vector.quantize_mx(out=zc[:].bitcast(FP8X4), scales=zs[:], in_=grouped.pop(g)[:].rearrange("p m t -> p (m t)"))
             z_codes[g] = (zc, zs)
 
-        def multiply(acc, g, codes, first, width):
+        def multiply(acc, g, codes, first, width, tts=(0, 1, 2, 3)):
             zc, zs = z_codes[g]
             wc, ws = codes
-            for tt in range(4):
+            for tt in tts:
                 nc.tensor.matmul_mx(
                     out=acc[tt][:, 0:width],
                     lhsT=zc[:, P * tt:P * tt + P].bitcast(FP8X4),
@@ -365,8 +365,9 @@ def tile_shiftedpatchtokenization_pa_kernel(tc, x, ln1_g, ln1_b, w1, b1, out):
             if n > FIRST:
                 quantise_w(n - 1)
                 codes = w_codes.pop(n - 1)
-                for h in range(2):
-                    multiply(narrow, 2 * (n - 1 - FIRST) + h, codes, N2 * h, N2)
+                for tts in ((0, 1, 2, 3),) if n < ITEMS else ((0,), (1,), (2,), (3,)):
+                    for h in range(2):
+                        multiply(narrow, 2 * (n - 1 - FIRST) + h, codes, N2 * h, N2, tts)
                 free_slots.append(codes)
             if FIRST <= n < FIRST + 4:
                 finish(wide, 0, N1, (n - FIRST,))

from contextlib import ExitStack

import concourse.mybir as mybir
from concourse.masks import make_identity

F32 = mybir.dt.float32
BF16 = mybir.dt.bfloat16
U32 = mybir.dt.uint32
U8 = mybir.dt.uint8
FP8X4 = mybir.dt.float8_e4m3fn_x4
ALU = mybir.AluOpType
ACT = mybir.ActivationFunctionType
AX = mybir.AxisListType

P = 128
B, C, HW, DIM = 8, 8, 128, 768
PD = 10240
EPS = 1e-5
FLOPS = 2 * B * 64 * PD * DIM
SHIFTS = ((0, 0), (-1, -1), (-1, 1), (1, -1), (1, 1))
PASSES = 20
N1, N2 = 512, 256
ITEMS = 30
FIRST = 20
HEAD_ITEMS = 7
SLOTS = 22
TILES = 32
LEAD_TILES = 8


def tile_shiftedpatchtokenization_pa_kernel(tc, x, ln1_g, ln1_b, w1, b1, out):
    nc = tc.nc
    with ExitStack() as ctx:
        ctx.enter_context(tc.manual_schedule())
        consts = ctx.enter_context(tc.tile_pool(name="consts", bufs=1))
        wraw_pool = ctx.enter_context(tc.tile_pool(name="wraw", bufs=5))
        wi_pool = ctx.enter_context(tc.tile_pool(name="wi", bufs=5))
        xh_pool = ctx.enter_context(tc.tile_pool(name="xh", bufs=12))
        zp_pool = ctx.enter_context(tc.tile_pool(name="zp", bufs=2))
        zi_pool = ctx.enter_context(tc.tile_pool(name="zi", bufs=2))
        acc_pool = ctx.enter_context(tc.psum_pool(name="acc", bufs=1))
        tp_pool = ctx.enter_context(tc.psum_pool(name="tp", bufs=4))

        w_raw, w_grouped, w_codes = {}, {}, {}
        free_slots = [
            (consts.tile([P, 512], U32, name="codes%d" % n, align_bytes=64), consts.tile([P, 512], U8, name="scales%d" % n, align_bytes=64))
            for n in range(SLOTS)
        ]

        def load_w(n):
            if n < FIRST:
                wr = wraw_pool.tile([P, 2048], BF16, name="wr")
                nc.sync.dma_start(
                    out=wr[:].rearrange("p (t n) -> p t n", t=4), in_=w1[512 * n:512 * n + 512, 0:N1].rearrange("(p t) n -> p t n", t=4)
                )
            else:
                wr = xh_pool.tile([P, 2048], BF16, name="xh")
                for h in range(2):
                    g = 2 * (n - FIRST) + h
                    nc.sync.dma_start(
                        out=wr[:, 1024 * h:1024 * h + 1024].rearrange("p (t n) -> p t n", t=4),
                        in_=w1[512 * g:512 * g + 512, N1:DIM].rearrange("(p t) n -> p t n", t=4),
                    )
            w_raw[n] = wr

        def regroup4(copy, dst, src):
            copy(out=dst.rearrange("p (c i) t -> p c t i", i=8), in_=src.rearrange("p t (c i) -> p c t i", i=8))

        def regroup_w_gpsimd(n):
            wr = w_raw.pop(n)[:].rearrange("p (t n) -> p t n", t=4)
            wi = wi_pool.tile([P, 512, 4], BF16, name="wi", align_bytes=64)
            for lo in range(0, 512, 128):
                nc.gpsimd.tensor_scalar(
                    out=wi[:, lo:lo + 128, :], in0=wr[:, :, lo:lo + 128].rearrange("p t n -> p n t"),
                    scalar1=1.0, scalar2=0.0, op0=ALU.mult, op1=ALU.add,
                )
            w_grouped[n] = wi
            load_w(n + 5)

        def regroup_w(n, scalar_cols):
            wr = w_raw.pop(n)
            wi = wi_pool.tile([P, 512, 4], BF16, name="wi", align_bytes=64)
            width = N1 if n < FIRST else N2
            for copy, start, stop in ((nc.scalar.copy, 512 - scalar_cols, 512), (nc.vector.tensor_copy, 0, 512 - scalar_cols)):
                for first in range(0, 512, width):
                    lo, hi = max(start, first), min(stop, first + width)
                    if lo < hi:
                        part = wr[:, 4 * first:4 * first + 4 * width].rearrange("p (t n) -> p t n", t=4)
                        regroup4(copy, wi[:, lo:hi, :], part[:, :, lo - first:hi - first])
            w_grouped[n] = wi
            if n + 5 < FIRST:
                load_w(n + 5)

        def quantise_w(n):
            wc, ws = free_slots.pop(0)
            nc.vector.quantize_mx(out=wc[:].bitcast(FP8X4), scales=ws[:], in_=w_grouped.pop(n)[:].rearrange("p n t -> p (n t)"))
            w_codes[n] = (wc, ws)

        one = consts.tile([P, 1], F32, name="one")
        nc.vector.memset(one[:], 1.0)
        nc.scalar.activation(out=one[:], in_=one[:], func=ACT.Abs_reciprocal_sqrt)

        gb = consts.tile([P, 512], BF16, name="gb")
        nc.vector.memset(gb[:], 0.0)
        nc.scalar.dma_start(out=gb[0:20, :], in_=ln1_g.rearrange("(r k) -> r k", k=512))
        nc.scalar.dma_start(out=gb[32:52, :], in_=ln1_b.rearrange("(r k) -> r k", k=512))
        xr = consts.tile([P, 4, 32, HW], BF16, name="xr")
        load_w(0)
        for c in (0, 2):
            for half in range(4):
                for b in (half, half + 4):
                    nc.sync.dma_start(
                        out=xr[b:b + 121:8, c:c + 2, 8:24, :].rearrange("p c r w -> p c (r w)"),
                        in_=x[b].rearrange("(c o) (i q) w -> (o i) c (q w)", o=2, i=8)[:, c:c + 2, :],
                    )
        for n in range(1, 5):
            load_w(n)
        b1b = consts.tile([P, DIM], BF16, name="b1b")

        eye = consts.tile([P, P], F32, name="eye")
        make_identity(nc, eye[:])
        nc.gpsimd.memset(xr[:, :, 24:32, :], 0.0)
        perm = consts.tile([P, P], F32, name="perm")
        nc.vector.tensor_copy(
            out=perm[:].rearrange("p (o b i) -> p o b i", o=2, b=8), in_=eye[:].rearrange("p (o i b) -> p o b i", o=2, i=8)
        )
        rot_dn = consts.tile([P, 2, 64], BF16, name="rot_dn")
        nc.vector.memset(rot_dn[:], 0.0)
        eye2 = eye[:].rearrange("p (o m) -> p o m", o=2)
        nc.vector.tensor_copy(out=rot_dn[:, :, 8:64], in_=eye2[:, :, 0:56])
        same = consts.tile([P, 2, 64], F32, name="same")
        upper = consts.tile([P, 2, 64], F32, name="upper")
        lower = consts.tile([P, 2, 64], F32, name="lower")
        for o in range(2):
            nc.vector.tensor_add(out=same[:, o, :], in0=eye2[:, 0, :], in1=eye2[:, 1, :])
        nc.vector.tensor_copy(out=upper[:], in_=same[:])
        nc.vector.tensor_copy(out=lower[:], in_=same[:])
        nc.vector.tensor_add(out=upper[:, :, 0:56], in0=upper[:, :, 0:56], in1=same[:, :, 8:64])
        nc.vector.tensor_add(out=lower[:, :, 8:64], in0=lower[:, :, 8:64], in1=same[:, :, 0:56])
        weights = consts.tile([P, 2, 2, P], F32, name="weights")
        cells = consts.tile([P, 2, 2, 18], F32, name="cells")
        nc.vector.memset(cells[:], 0.0)
        for a, rows in enumerate((upper, lower)):
            flat = rows[:].rearrange("p o m -> p (o m)")
            nc.vector.tensor_scalar_mul(out=weights[:, 0, a, :], in0=flat, scalar1=64.0 / PD)
            nc.vector.scalar_tensor_tensor(
                out=weights[:, 1, a, :], in0=same[:].rearrange("p o m -> p (o m)"), scalar=64.0 / PD, in1=weights[:, 0, a, :], op0=ALU.mult, op1=ALU.add
            )

        regroup_w(0, 256)

        st6 = consts.tile([P, 2, 16, 2, 6], F32, name="st6")

        def cell_stats(h):
            for a in range(2):
                for j in range(16):
                    nc.vector.bn_stats(out=st6[:, a, j, h, :], in_=xr[:, 2 * h:2 * h + 2, 8 + 8 * a:16 + 8 * a, 8 * j:8 * j + 8])

        def neighbours(c, dst, rot, row):
            ps = tp_pool.tile([P, 1024], BF16, name="tp")
            rows = xr[:, c, row:row + 8, :].rearrange("p r w -> p (r w)")
            for h in range(2):
                nc.tensor.matmul(
                    out=ps[:, 512 * h:512 * h + 512], lhsT=rot[:].rearrange("p o m -> p (o m)"), rhs=rows[:, 512 * h:512 * h + 512],
                    start=True, stop=True,
                )
            nc.scalar.copy(out=xr[:, c, dst:dst + 8, :].rearrange("p r w -> p (r w)"), in_=ps[:])

        cell_stats(0)
        for c in range(2):
            neighbours(c, 0, rot_dn, 16)
        cell_stats(1)
        for c in range(2, 4):
            neighbours(c, 0, rot_dn, 16)
        regroup_w_gpsimd(1)
        regroup_w_gpsimd(2)
        for n in (3, 4, 5):
            regroup_w(n, 512)
        groups = st6[:].rearrange("p a j h (e k) -> p a j (h e) k", e=2)
        sqm = consts.tile([P, 2, 16, 4], F32, name="sqm")
        s2 = consts.tile([P, 2, 16], F32, name="s2")
        m2 = consts.tile([P, 2, 16], F32, name="m2")
        nc.vector.tensor_mul(out=sqm[:], in0=groups[:, :, :, :, 1], in1=groups[:, :, :, :, 1])
        nc.vector.tensor_reduce(out=m2[:], in_=groups[:, :, :, :, 2], axis=AX.X, op=ALU.add)
        nc.vector.tensor_reduce(out=s2[:], in_=sqm[:], axis=AX.X, op=ALU.add)
        nc.vector.tensor_reduce(out=cells[:, :, 0, 1:17], in_=groups[:, :, :, :, 1], axis=AX.X, op=ALU.add)
        nc.vector.scalar_tensor_tensor(out=cells[:, :, 1, 1:17], in0=m2[:], scalar=1.0 / 64, in1=s2[:], op0=ALU.mult, op1=ALU.add)
        columns = consts.tile([P, 2, 2, 2, 8], F32, name="columns")
        nc.vector.tensor_add(out=columns[:, 0, :, :, :], in0=cells[:, :, :, 0:16:2], in1=cells[:, :, :, 3:18:2])
        nc.vector.tensor_add(out=columns[:, 1, :, :, :], in0=cells[:, :, :, 1:17:2], in1=cells[:, :, :, 2:18:2])
        st = tp_pool.tile([P, 2, 8], F32, name="tp")
        for n in range(4):
            nc.tensor.matmul(
                out=st[:].rearrange("p s j -> p (s j)"),
                lhsT=weights[:, n // 2, n % 2, :],
                rhs=columns[:, n // 2, n % 2, :, :].rearrange("p s j -> p (s j)"),
                start=(n == 0),
                stop=(n == 3),
            )
        gk = consts.tile([P, 4, PASSES], F32, name="gk")
        bk = consts.tile([P, 4, PASSES], F32, name="bk")
        gb_t = consts.tile([P, 4, P], F32, name="gb_t")
        nc.vector.tensor_copy(out=gb_t[:], in_=gb[:].rearrange("r (p t) -> r t p", t=4))
        pt = tp_pool.tile([P, 4, P], F32, name="tp")
        for t in range(4):
            nc.tensor.transpose(out=pt[:, t, :], in_=gb_t[:, t, :], identity=eye[:])

        quantise_w(0)
        tot = consts.tile([P, 2, 8], F32, name="tot")
        small = {}
        for nm in ("msq", "var", "r0", "nt", "rstd", "nmr"):
            small[nm] = consts.tile([P, 8], F32, name=nm)
        msq, var, r0, nt, rstd, nmr = (small[nm] for nm in ("msq", "var", "r0", "nt", "rstd", "nmr"))
        nc.vector.tensor_copy(out=tot[:], in_=st[:])
        nc.vector.tensor_mul(out=msq[:], in0=tot[:, 0, :], in1=tot[:, 0, :])
        nc.vector.scalar_tensor_tensor(out=var[:], in0=tot[:, 1, :], scalar=EPS, in1=msq[:], op0=ALU.add, op1=ALU.subtract)
        nc.vector.tensor_scalar_max(out=var[:], in0=var[:], scalar1=EPS)
        nc.scalar.activation(out=r0[:], in_=var[:], func=ACT.Abs_reciprocal_sqrt)
        quantise_w(1)
        regroup_w(6, 512)
        nc.vector.scalar_tensor_tensor(out=nt[:], in0=r0[:], scalar=-0.5, in1=r0[:], op0=ALU.mult, op1=ALU.mult)
        nc.vector.tensor_mul(out=nt[:], in0=nt[:], in1=var[:])
        nc.vector.scalar_tensor_tensor(out=rstd[:], in0=nt[:], scalar=1.5, in1=r0[:], op0=ALU.add, op1=ALU.mult)
        nc.vector.scalar_tensor_tensor(out=nmr[:], in0=tot[:, 0, :], scalar=-1.0, in1=rstd[:], op0=ALU.mult, op1=ALU.mult)

        nc.vector.tensor_copy(out=gk[:], in_=pt[:, :, 0:20])
        nc.vector.tensor_copy(out=bk[:], in_=pt[:, :, 32:52])

        def affine(on_scalar, dst, src, scale, bias):
            if on_scalar:
                nc.scalar.activation(out=dst, in_=src, func=ACT.Identity, bias=bias, scale=scale)
            else:
                nc.vector.tensor_scalar(out=dst, in0=src, scalar1=scale, scalar2=bias, op0=ALU.mult, op1=ALU.add)

        xh_tiles = {}
        edge_tiles = {(j, n): consts.tile([P, 1280], F32, name="edge%d%d" % (j, n)) for j in (0, 7) for n in range(2)}

        def normalise(k, n_scalar):
            j = k % 8
            row0 = 8 + 4 * (k // 8)
            xh = edge_tiles[j, (k // 8) % 2] if j in (0, 7) else xh_pool.tile([P, 1280], F32, name="xh")
            view = xh[:].rearrange("p (q e s c) -> p q e s c", q=4, e=16, s=5)
            for s, (di, dj) in enumerate(SHIFTS):
                col0 = 16 * j + 8 * dj
                lo = 8 if col0 < 0 else 0
                hi = 8 if col0 + 16 > HW else 16
                on_scalar = s >= 5 - n_scalar
                src = xr[:, :, row0 + 8 * di:row0 + 8 * di + 4, col0 + lo:col0 + hi].rearrange("p c q e -> p q e c")
                affine(on_scalar, view[:, :, lo:hi, s, :], src, rstd[:, j:j + 1], nmr[:, j:j + 1])
                if hi - lo < 16 and k < 16:
                    affine(on_scalar, view[:, :, 8 - lo:24 - hi, s, :], src, 0.0, nmr[:, j:j + 1])
            xh_tiles[k] = xh

        banks, planes, grouped, z_codes = {}, {}, {}, {}

        def transposes(g):
            banks[g] = {}
            for jg in range(2):
                for t2 in range(2):
                    pt = tp_pool.tile([P, 4, P], F32, name="tp")
                    for jj in range(4):
                        lo = 256 * (g % 5) + t2
                        xh = xh_tiles[8 * (g // 5) + 4 * jg + jj]
                        nc.tensor.transpose(out=pt[:, jj, :], in_=xh[:, lo:lo + 255:2], identity=perm[:])
                    banks[g][jg, t2] = pt

        def evacuate(g):
            zp = zp_pool.tile([P, 4, 512], BF16, name="zp")
            for (jg, t2), pt in banks.pop(g).items():
                for o in range(2):
                    t = 2 * t2 + o
                    affine(True, zp[:, t, 256 * jg:256 * jg + 256].rearrange("p (j m) -> p j m", j=4), pt[:, :, 64 * o:64 * o + 64],
                           gk[:, t, g:g + 1], bk[:, t, g:g + 1])
            planes[g] = zp

        def regroup_z(g):
            zi = zi_pool.tile([P, 512, 4], BF16, name="zi", align_bytes=64)
            regroup4(nc.vector.tensor_copy, zi[:], planes.pop(g)[:])
            grouped[g] = zi

        def quantise_z(g):
            zc, zs = free_slots.pop(0)
            nc.vector.quantize_mx(out=zc[:].bitcast(FP8X4), scales=zs[:], in_=grouped.pop(g)[:].rearrange("p m t -> p (m t)"))
            z_codes[g] = (zc, zs)

        def multiply(acc, g, codes, first, width, tts=(0, 1, 2, 3)):
            zc, zs = z_codes[g]
            wc, ws = codes
            for tt in tts:
                nc.tensor.matmul_mx(
                    out=acc[tt][:, 0:width],
                    lhsT=zc[:, P * tt:P * tt + P].bitcast(FP8X4),
                    lhsT_scale=zs[:, P * tt:P * tt + P],
                    rhs=wc[:, first:first + width].bitcast(FP8X4),
                    rhs_scale=ws[:, first:first + width],
                    start=(g == 0),
                    stop=(g == PASSES - 1),
                )

        out_rows = out.rearrange("b (i j) n -> j (b i) n", j=8)

        def finish(acc, first, width, tts):
            for tt in tts:
                o = wraw_pool.tile([P, N1], F32, name="wr")
                nc.vector.tensor_tensor(out=o[:, 0:width], in0=acc[tt][:, 0:width], in1=b1b[:, first:first + width], op=ALU.add)
                for jl in range(2):
                    nc.sync.dma_start(out=out_rows[2 * tt + jl][:, first:first + width], in_=o[64 * jl:64 * jl + 64, 0:width])

        wide, narrow = {}, {}
        for tt in range(4):
            wide[tt] = acc_pool.tile([P, N1], F32, name="acc%d" % tt)
        for k in range(LEAD_TILES):
            normalise(k, 2 if k < 4 else 1)
        made = LEAD_TILES
        for n in range(2, HEAD_ITEMS):
            quantise_w(n)
        next_item = HEAD_ITEMS
        regrouped = []
        next_load = FIRST
        for o in range(2):
            for c in range(4):
                nc.sync.dma_start(
                    out=xr[64 * o:64 * o + 56, c, 24:32, :].rearrange("p r w -> p (r w)"),
                    in_=x[:, 2 * c + o, :, :].rearrange("b (i q) w -> i b (q w)", q=16)[1:8, :, 0:1024],
                )
        for step in range(PASSES + 3):
            if 1 <= step < PASSES + 1:
                evacuate(step - 1)
            if 2 <= step < PASSES + 2:
                regroup_z(step - 2)
            items = range(next_item, min(HEAD_ITEMS + (step + 1) // 2 + max(0, step - 15), FIRST))
            next_item += len(items)
            for n in items:
                regroup_w(n, 208)
            for n in regrouped:
                quantise_w(n)
            regrouped = items
            if 2 <= step < PASSES + 2:
                quantise_z(step - 2)
            if step == 8:
                nc.sync.dma_start(out=b1b[:], in_=b1.partition_broadcast(P))
            if step >= 3:
                codes = w_codes.pop(step - 3)
                multiply(wide, step - 3, codes, 0, N1)
                free_slots.append(codes)
            if step < PASSES:
                transposes(step)
            target = min(TILES, LEAD_TILES + (8 * (step + 1)) // 5)
            while made < target:
                normalise(made, 1)
                made += 1
            if step in (15, 16):
                for n in range(next_load, next_load + 3):
                    load_w(n)
                next_load += 3
        while next_load < ITEMS:
            load_w(next_load)
            next_load += 1

        for tt in range(4):
            narrow[tt] = tp_pool.tile([P, N2], F32, name="tp")
        for n in range(FIRST, ITEMS + 1):
            if n < ITEMS:
                regroup_w(n, 352 if n < FIRST + 4 else 304)
            if n > FIRST:
                quantise_w(n - 1)
                codes = w_codes.pop(n - 1)
                for tts in ((0, 1, 2, 3),) if n < ITEMS else ((0,), (1,), (2,), (3,)):
                    for h in range(2):
                        multiply(narrow, 2 * (n - 1 - FIRST) + h, codes, N2 * h, N2, tts)
                free_slots.append(codes)
            if FIRST <= n < FIRST + 4:
                finish(wide, 0, N1, (n - FIRST,))
        finish(narrow, N1, N2, range(4))
